import numpy as np
import ml_dtypes


def mxq(x, axis, fmt="e4m3"):
    dtype, down = {"e4m3": (ml_dtypes.float8_e4m3fn, 7), "e5m2": (ml_dtypes.float8_e5m2, 14)}[fmt]
    v = np.moveaxis(np.asarray(x, np.float32).astype(ml_dtypes.bfloat16).astype(np.float64), axis, -1)
    blocks = v.reshape(v.shape[:-1] + (-1, 32))
    amax = np.abs(blocks).max(-1, keepdims=True)
    byte = np.maximum(np.where(amax > 0, np.frexp(amax)[1] - 1 + 127, 0) - down, 1)
    scale = np.exp2(byte - 127.0)
    codes = (blocks / scale).astype(np.float32).astype(dtype).astype(np.float64)
    return np.moveaxis((codes * scale).reshape(v.shape), -1, axis)


WIDE = False


def mx_kscale(k):
    if not WIDE:
        return np.ones(k)
    levels = np.array([10, -10, 5, -5, 0])
    a = np.random.permutation(np.resize(levels, k // 512 * 4)).reshape(k // 512, 4)
    idx = np.arange(k)
    return np.exp2(a[idx // 512, idx % 128 // 32])


BF16 = ml_dtypes.bfloat16


def bf(x):
    return np.asarray(x, np.float32).astype(BF16)


def f64(x):
    return np.asarray(x).astype(np.float64)


E2M1 = np.array([0.0, 0.5, 1.0, 1.5, 2.0, 3.0, 4.0, 6.0, -0.0, -0.5, -1.0, -1.5, -2.0, -3.0, -4.0, -6.0])


def pack_weight(w, fmt):
    k, n = w.shape
    w = f64(bf(w)).reshape(k // 32, 32, n)
    amax = np.abs(w).max(1)
    if fmt == "e4m3":
        byte = np.frexp(amax)[1] - 1 + 127 - 7
    else:
        mant, ex = np.frexp(amax / 6.0)
        byte = np.where(mant > 0.5, ex, ex - 1) + 127
    byte = np.clip(np.where(amax > 0, byte, 1), 1, 254)
    scaled = (w * np.exp2(127.0 - byte)[:, None, :]).reshape(k, n).astype(np.float32)
    by_word = np.ascontiguousarray(scaled.reshape(k // 512, 128, 4, n).transpose(0, 1, 3, 2))
    if fmt == "e4m3":
        words = by_word.astype(ml_dtypes.float8_e4m3fn).view(np.uint8)
    else:
        c = by_word.astype(ml_dtypes.float4_e2m1fn).view(np.uint8) & 0xF
        words = c[..., 0::2] | (c[..., 1::2] << 4)
    return np.ascontiguousarray(words), np.ascontiguousarray(byte.astype(np.uint8).reshape(k // 512, 16, n))


def unpack_weight(words, scales, fmt):
    g, p, n, _ = words.shape
    if fmt == "e4m3":
        vals = np.ascontiguousarray(words).view(ml_dtypes.float8_e4m3fn).astype(np.float64)
    else:
        nib = np.empty((g, p, n, 4), np.uint8)
        nib[..., 0::2] = words & 0xF
        nib[..., 1::2] = words >> 4
        vals = E2M1[nib]
    vals = vals * np.repeat(np.exp2(scales.astype(np.float64) - 127.0), 8, axis=1)[..., None]
    return vals.transpose(0, 1, 3, 2).reshape(g * 512, n)


NQ, NK, QS, KS, F, DEG = 512, 1024, 16384, 512, 512, 32
EPS = 1e-5
SLOPE = 0.01
FMT = "e4m3"


def leaky(v):
    return np.where(v >= 0, v, SLOPE * v)


def setup_inputs():
    s, t = mx_kscale(QS), mx_kscale(F)
    x = bf(np.random.standard_normal((NQ, QS)) * s)
    w1_words, w1_scales = pack_weight(np.random.standard_normal((QS, F)) / np.sqrt(QS) / s[:, None] * t, FMT)
    b1 = bf(np.random.standard_normal(F) * 0.5 * t)
    w2_words, w2_scales = pack_weight(np.random.standard_normal((F, F)) / np.sqrt(F) / t[:, None], FMT)
    b2 = bf(np.random.standard_normal(F) * 0.5)
    gamma = bf(1.0 + 0.1 * np.random.standard_normal(F))
    beta = bf(0.1 * np.random.standard_normal(F))
    return {"x": x,
            "w1_words": w1_words,
            "w1_scales": w1_scales,
            "b1": b1,
            "w2_words": w2_words,
            "w2_scales": w2_scales,
            "b2": b2,
            "gamma": gamma,
            "beta": beta}


def reference(x, w1_words, w1_scales, b1, w2_words, w2_scales, b2, gamma, beta):
    h = leaky((mxq(f64(x), 1, "e4m3") @ unpack_weight(w1_words, w1_scales, FMT)) + f64(b1))
    h = leaky((mxq(h, 1, "e4m3") @ unpack_weight(w2_words, w2_scales, FMT)) + f64(b2))
    mean = h.mean(axis=0)
    var = h.var(axis=0)
    return f64(gamma) * (h - mean) / np.sqrt(var + EPS) + f64(beta)

@@ -1,0 +1,322 @@
+from contextlib import ExitStack
+
+import concourse.mybir as mybir
+from concourse.masks import make_identity
+
+BF16 = mybir.dt.bfloat16
+F32 = mybir.dt.float32
+I32 = mybir.dt.int32
+U32 = mybir.dt.uint32
+U8 = mybir.dt.uint8
+FP8X4 = mybir.dt.float8_e4m3fn_x4
+ALU = mybir.AluOpType
+ACT = mybir.ActivationFunctionType
+
+P = 128
+PACK = 4
+K_PASS = P * PACK
+ROWS, K1, FEATS = 512, 16384, 512
+ROW_TILES = ROWS // P
+FEAT_TILES = FEATS // P
+SPAN_PASSES = 4
+SPAN_K = SPAN_PASSES * K_PASS
+SPANS = K1 // SPAN_K
+LAST_SPANS = 2
+RUN_TILES = 2
+X_BUFS = 12
+QUADRANTS = 4
+SLOPE = 0.01
+EPS = 1e-5
+BN_STATS = 6
+
+FLOPS = 2 * ROWS * K1 * FEATS + 2 * ROWS * FEATS * FEATS
+
+
+def tile_attention_prop_pa_k_kernel(
+    tc, x, w1_words, w1_scales, b1, w2_words, w2_scales, b2, gamma, beta, out
+):
+    nc = tc.nc
+
+    first_spans = SPANS - LAST_SPANS
+    order = [(a, s) for s in range(first_spans) for a in range(ROW_TILES)]
+    order += [(a, s) for a in range(ROW_TILES) for s in range(first_spans, SPANS)]
+    runs = [list(range(n, n + RUN_TILES)) for n in range(0, len(order), RUN_TILES)]
+    weights_behind = {}
+    spans_seen = []
+    for n, (a, s) in enumerate(order):
+        if s not in spans_seen:
+            spans_seen.append(s)
+            last_of_run = runs[n // RUN_TILES][-1]
+            weights_behind[last_of_run] = weights_behind.get(last_of_run, []) + [s]
+
+    def tiles_of(r):
+        return runs[r] if 0 <= r < len(runs) else []
+
+    def closed_in(r):
+        return [order[n][0] for n in tiles_of(r) if order[n][1] == SPANS - 1]
+
+    with ExitStack() as ctx:
+        const = ctx.enter_context(tc.tile_pool(name="const", bufs=1))
+        x_pool = ctx.enter_context(tc.tile_pool(name="x", bufs=X_BUFS))
+        sorted_pool = ctx.enter_context(tc.tile_pool(name="sorted", bufs=2 * RUN_TILES))
+        grouped_pool = ctx.enter_context(tc.tile_pool(name="grouped", bufs=2 * RUN_TILES))
+        codes_pool = ctx.enter_context(tc.tile_pool(name="codes", bufs=3 * RUN_TILES))
+        tail = ctx.enter_context(tc.tile_pool(name="tail", bufs=2))
+        sums = ctx.enter_context(tc.psum_pool(name="sums", bufs=1))
+        banks = ctx.enter_context(tc.psum_pool(name="banks", bufs=4))
+        ctx.enter_context(tc.manual_schedule())
+
+        w1_tiles = [
+            const.tile([P, SPAN_PASSES, PACK * FEATS], U8, name="w1_span%d" % s, align_bytes=64)
+            for s in range(SPANS)
+        ]
+        w1_planes = [
+            const.tile([P, FEATS], U8, name="w1_planes%d" % s, align_bytes=64)
+            for s in range(SPANS)
+        ]
+        w2_tile = const.tile([P, PACK * FEATS], U8, name="w2_tile", align_bytes=64)
+        w2_plane = const.tile([P, FEATS], U8, name="w2_plane", align_bytes=64)
+        ident_f32 = const.tile([P, P], F32, name="ident_f32")
+        ident_bf16 = const.tile([P, P], BF16, name="ident_bf16")
+        ones = const.tile([P, P], BF16, name="ones")
+        b1_row = const.tile([P, FEATS], BF16, name="b1_row")
+        b1_all = const.tile([P, FEATS], F32, name="b1_all")
+        vec_rows = const.tile([P, P], BF16, name="vec_rows")
+        vec_cols = const.tile([P, 3 * FEAT_TILES], F32, name="vec_cols")
+        b2_cols = vec_cols[:, 0:FEAT_TILES]
+        gamma_cols = vec_cols[:, FEAT_TILES : 2 * FEAT_TILES]
+        beta_cols = vec_cols[:, 2 * FEAT_TILES : 3 * FEAT_TILES]
+        one_col = const.tile([P, 1], F32, name="one_col")
+        root_col = const.tile([P, 1], F32, name="root_col")
+        h1_grouped = const.tile([P, ROW_TILES, P, PACK], BF16, name="h1_grouped", align_bytes=64)
+        h1_codes = const.tile([P, ROWS], U32, name="h1_codes", align_bytes=64)
+        h1_scales = const.tile([P, ROWS], U8, name="h1_scales", align_bytes=64)
+        h2 = const.tile([P, FEAT_TILES, ROW_TILES, P], F32, name="h2")
+        stats = const.tile([P, FEAT_TILES, ROW_TILES, BN_STATS], F32, name="stats")
+        mean_var = const.tile([P, FEAT_TILES, 2], F32, name="mean_var")
+        var_eps = const.tile([P, FEAT_TILES], F32, name="var_eps")
+        std = const.tile([P, FEAT_TILES], F32, name="std")
+        rstd = const.tile([P, FEAT_TILES], F32, name="rstd")
+        gain = const.tile([P, FEAT_TILES], F32, name="gain")
+        mean_gain = const.tile([P, FEAT_TILES], F32, name="mean_gain")
+        shift = const.tile([P, FEAT_TILES], F32, name="shift")
+        acc = [
+            sums.tile([P, FEATS], F32, name="acc%d" % a, tag="sum%d" % a) for a in range(ROW_TILES)
+        ]
+
+        x_tiles, sorted_tiles, grouped_tiles, code_tiles, h1_tiles, h2_banks = {}, {}, {}, {}, {}, {}
+
+        def load_scale_rows(plane, rows_per_quadrant, scale_rows):
+            for quadrant in range(QUADRANTS):
+                first = 32 * quadrant
+                nc.sync.dma_start(
+                    out=plane[first : first + rows_per_quadrant, :].bitcast(I32),
+                    in_=scale_rows(quadrant).bitcast(I32),
+                )
+
+        def load_x_tile(n):
+            a, s = order[n]
+            x_tiles[n] = x_pool.tile([P, SPAN_K], BF16, name="x_tile")
+            nc.sync.dma_start(
+                out=x_tiles[n][:], in_=x[a * P : (a + 1) * P, s * SPAN_K : (s + 1) * SPAN_K]
+            )
+            for span in weights_behind.get(n, []):
+                load_span_weights(span)
+
+        def load_span_weights(s):
+            groups = slice(s * SPAN_PASSES, (s + 1) * SPAN_PASSES)
+            load_scale_rows(
+                w1_planes[s],
+                4 * SPAN_PASSES,
+                lambda quadrant: w1_scales[groups, 4 * quadrant : 4 * quadrant + 4, :],
+            )
+            nc.sync.dma_start(
+                out=w1_tiles[s][:].bitcast(I32),
+                in_=w1_words[groups].rearrange("g p n t -> p g (n t)").bitcast(I32),
+            )
+
+        def sort_words(n):
+            sorted_tiles[n] = sorted_pool.tile([P, SPAN_PASSES, 2, P], F32, name="sorted_words")
+            nc.vector.tensor_copy(
+                out=sorted_tiles[n][:],
+                in_=x_tiles[n][:]
+                .bitcast(F32)
+                .rearrange("p (j w u) -> p j u w", j=SPAN_PASSES, u=2),
+            )
+            if n + X_BUFS < len(order):
+                load_x_tile(n + X_BUFS)
+
+        def transpose_x(n):
+            grouped_tiles[n] = grouped_pool.tile([P, SPAN_K], BF16, name="grouped", align_bytes=64)
+            words = grouped_tiles[n][:].bitcast(F32).rearrange(
+                "p (j m u) -> p j m u", j=SPAN_PASSES, u=2
+            )
+            for half in range(SPAN_PASSES // 2):
+                bank = banks.tile([P, 2, 2, P], F32, name="x_bank", tag="bank")
+                for jj in range(2):
+                    for u in range(2):
+                        nc.tensor.transpose(
+                            out=bank[:, jj, u, :],
+                            in_=sorted_tiles[n][:, 2 * half + jj, u, :],
+                            identity=ident_f32[:],
+                        )
+                nc.scalar.copy(
+                    out=words[:, 2 * half : 2 * half + 2],
+                    in_=bank[:].rearrange("p j u m -> p j m u"),
+                )
+
+        def quantise_x(n):
+            codes = codes_pool.tile([P, SPAN_PASSES * P], U32, name="x_codes", align_bytes=64)
+            scales = codes_pool.tile([P, SPAN_PASSES * P], U8, name="x_scales", align_bytes=64)
+            nc.vector.quantize_mx(
+                out=codes[:].bitcast(FP8X4), scales=scales[:], in_=grouped_tiles[n][:]
+            )
+            code_tiles[n] = (codes, scales)
+
+        def first_layer_passes(n):
+            a, s = order[n]
+            codes, scales = code_tiles[n]
+            for j in range(SPAN_PASSES):
+                rows = slice(j * P, (j + 1) * P)
+                nc.tensor.matmul_mx(
+                    out=acc[a][:],
+                    lhsT=codes[:, rows].bitcast(FP8X4),
+                    lhsT_scale=scales[:, rows],
+                    rhs=w1_tiles[s][:, j, :].bitcast(FP8X4),
+                    rhs_scale=w1_planes[s][4 * j : P, :],
+                    start=(s == 0 and j == 0),
+                    stop=(s == SPANS - 1 and j == SPAN_PASSES - 1),
+                )
+
+        def hidden_values(a):
+            biased = tail.tile([P, FEATS], F32, name="biased")
+            nc.vector.tensor_tensor(out=biased[:], in0=acc[a][:], in1=b1_all[:], op=ALU.add)
+            h1_tiles[a] = tail.tile([P, FEATS], BF16, name="h1_rows")
+            nc.vector.scalar_tensor_tensor(
+                out=h1_tiles[a][:], in0=biased[:], scalar=SLOPE, in1=biased[:],
+                op0=ALU.mult, op1=ALU.max,
+            )
+
+        def transpose_hidden(a):
+            bank = banks.tile([P, PACK, P], BF16, name="h1_bank", tag="bank")
+            for t in range(PACK):
+                nc.tensor.transpose(
+                    out=bank[:, t, :], in_=h1_tiles[a][:, t:FEATS:PACK], identity=ident_bf16[:]
+                )
+            nc.scalar.copy(out=h1_grouped[:, a], in_=bank[:].rearrange("p t m -> p m t"))
+
+        def quantise_hidden(a):
+            rows = slice(a * P, (a + 1) * P)
+            nc.vector.quantize_mx(
+                out=h1_codes[:, rows].bitcast(FP8X4),
+                scales=h1_scales[:, rows],
+                in_=h1_grouped[:, a].rearrange("p m t -> p (m t)"),
+            )
+
+        def second_layer(a):
+            rows = slice(a * P, (a + 1) * P)
+            bank = sums.tile([P, FEAT_TILES, P], F32, name="h2_bank", tag="sum%d" % a)
+            biased = tail.tile([P, FEAT_TILES, P], F32, name="h2_biased")
+            for j in range(FEAT_TILES):
+                nc.tensor.matmul_mx(
+                    out=bank[:, j, :],
+                    lhsT=w2_tile[:, j * PACK * P : (j + 1) * PACK * P].bitcast(FP8X4),
+                    lhsT_scale=w2_plane[:, j * P : (j + 1) * P],
+                    rhs=h1_codes[:, rows].bitcast(FP8X4),
+                    rhs_scale=h1_scales[:, rows],
+                    start=True,
+                    stop=True,
+                )
+                nc.scalar.activation(
+                    out=biased[:, j, :], in_=bank[:, j, :], func=ACT.Identity,
+                    bias=b2_cols[:, j : j + 1], scale=1.0,
+                )
+            h2_banks[a] = biased
+
+        def second_layer_statistics(a):
+            biased = h2_banks[a]
+            nc.vector.scalar_tensor_tensor(
+                out=h2[:, :, a, :], in0=biased[:], scalar=SLOPE, in1=biased[:],
+                op0=ALU.mult, op1=ALU.max,
+            )
+            for j in range(FEAT_TILES):
+                nc.vector.bn_stats(out=stats[:, j, a, :], in_=h2[:, j, a, :])
+
+        for plane in w1_planes + [w2_plane]:
+            nc.vector.memset(plane[:].bitcast(I32), 0)
+        nc.vector.memset(b1_row[:], 0.0)
+        nc.vector.memset(vec_rows[:], 0.0)
+        nc.vector.memset(ones[:], 1.0)
+        nc.vector.memset(one_col[:], 1.0)
+        make_identity(nc, ident_f32[:])
+        make_identity(nc, ident_bf16[:])
+
+        for n in range(X_BUFS):
+            load_x_tile(n)
+        load_scale_rows(w2_plane, 4, lambda quadrant: w2_scales[0, 4 * quadrant : 4 * quadrant + 4, :])
+        nc.sync.dma_start(
+            out=w2_tile[:].bitcast(I32),
+            in_=w2_words[0].rearrange("p n t -> p (n t)").bitcast(I32),
+        )
+
+        nc.scalar.dma_start(out=b1_row[0:1, :], in_=b1.rearrange("(o f) -> o f", o=1))
+        for i, vector in enumerate((b2, gamma, beta)):
+            nc.scalar.dma_start(
+                out=vec_rows[i * FEAT_TILES : (i + 1) * FEAT_TILES, :],
+                in_=vector.rearrange("(j p) -> j p", p=P),
+            )
+        nc.scalar.activation(out=root_col[:], in_=one_col[:], func=ACT.Sqrt)
+
+        b1_bank = banks.tile([P, FEATS], F32, name="b1_bank", tag="bank")
+        nc.tensor.matmul(out=b1_bank[:], lhsT=ones[:], rhs=b1_row[:], start=True, stop=True)
+        nc.scalar.copy(out=b1_all[:], in_=b1_bank[:])
+        vec_bank = banks.tile([P, P], BF16, name="vec_bank", tag="bank")
+        nc.tensor.transpose(out=vec_bank[:], in_=vec_rows[:], identity=ident_bf16[:])
+        nc.vector.tensor_copy(out=vec_cols[:], in_=vec_bank[:, 0 : 3 * FEAT_TILES])
+
+        for r in range(-2, len(runs) + 1):
+            for n in tiles_of(r + 2):
+                sort_words(n)
+            for n in tiles_of(r + 1):
+                transpose_x(n)
+            for a in closed_in(r - 1):
+                transpose_hidden(a)
+            for n in tiles_of(r + 1):
+                quantise_x(n)
+            for a in closed_in(r - 1):
+                quantise_hidden(a)
+            for n in tiles_of(r):
+                first_layer_passes(n)
+            for a in closed_in(r - 1):
+                second_layer(a)
+            for a in closed_in(r):
+                hidden_values(a)
+            for a in closed_in(r - 1):
+                second_layer_statistics(a)
+
+        for j in range(FEAT_TILES):
+            nc.vector.bn_aggr(
+                out=mean_var[:, j, :], in_=stats[:, j].rearrange("p a c -> p (a c)")
+            )
+        nc.vector.tensor_scalar(
+            out=var_eps[:], in0=mean_var[:, :, 1], scalar1=EPS, scalar2=None, op0=ALU.add
+        )
+        nc.scalar.activation(out=std[:], in_=var_eps[:], func=ACT.Sqrt)
+        nc.vector.reciprocal(out=rstd[:], in_=std[:])
+        nc.vector.tensor_tensor(out=gain[:], in0=gamma_cols, in1=rstd[:], op=ALU.mult)
+        nc.vector.tensor_tensor(out=mean_gain[:], in0=mean_var[:, :, 0], in1=gain[:], op=ALU.mult)
+        nc.vector.tensor_tensor(out=shift[:], in0=beta_cols, in1=mean_gain[:], op=ALU.subtract)
+
+        out_by_row_tile = out.rearrange("(a m) f -> m a f", m=P)
+        for j in range(FEAT_TILES):
+            normed = tail.tile([P, ROW_TILES, P], F32, name="normed")
+            nc.vector.tensor_scalar(
+                out=normed[:], in0=h2[:, j], scalar1=gain[:, j : j + 1], scalar2=shift[:, j : j + 1],
+                op0=ALU.mult, op1=ALU.add,
+            )
+            out_bank = sums.tile([P, ROW_TILES, P], F32, name="out_bank", tag="sum%d" % j)
+            for a in range(ROW_TILES):
+                nc.tensor.transpose(out=out_bank[:, a, :], in_=normed[:, a, :], identity=ident_f32[:])
+            out_rows = tail.tile([P, ROW_TILES, P], F32, name="out_rows")
+            nc.scalar.copy(out=out_rows[:], in_=out_bank[:])
+            nc.sync.dma_start(out=out_by_row_tile[:, :, j * P : (j + 1) * P], in_=out_rows[:])

@@ -58,7 +58,6 @@ def tile_attention_prop_pa_k_kernel(
     with ExitStack() as ctx:
         const = ctx.enter_context(tc.tile_pool(name="const", bufs=1))
         x_pool = ctx.enter_context(tc.tile_pool(name="x", bufs=X_BUFS))
-        sorted_pool = ctx.enter_context(tc.tile_pool(name="sorted", bufs=2 * RUN_TILES))
         grouped_pool = ctx.enter_context(tc.tile_pool(name="grouped", bufs=2 * RUN_TILES))
         codes_pool = ctx.enter_context(tc.tile_pool(name="codes", bufs=3 * RUN_TILES))
         tail = ctx.enter_context(tc.tile_pool(name="tail", bufs=2))
@@ -104,7 +103,7 @@ def tile_attention_prop_pa_k_kernel(
             sums.tile([P, FEATS], F32, name="acc%d" % a, tag="sum%d" % a) for a in range(ROW_TILES)
         ]
 
-        x_tiles, sorted_tiles, grouped_tiles, code_tiles, h1_tiles, h2_banks = {}, {}, {}, {}, {}, {}
+        x_tiles, grouped_tiles, code_tiles, h1_tiles, h2_banks = {}, {}, {}, {}, {}
 
         def load_scale_rows(plane, rows_per_quadrant, scale_rows):
             for quadrant in range(QUADRANTS):
@@ -135,21 +134,13 @@ def tile_attention_prop_pa_k_kernel(
                 in_=w1_words[groups].rearrange("g p n t -> p g (n t)").bitcast(I32),
             )
 
-        def sort_words(n):
-            sorted_tiles[n] = sorted_pool.tile([P, SPAN_PASSES, 2, P], F32, name="sorted_words")
-            nc.vector.tensor_copy(
-                out=sorted_tiles[n][:],
-                in_=x_tiles[n][:]
-                .bitcast(F32)
-                .rearrange("p (j w u) -> p j u w", j=SPAN_PASSES, u=2),
-            )
-            if n + X_BUFS < len(order):
-                load_x_tile(n + X_BUFS)
-
         def transpose_x(n):
             grouped_tiles[n] = grouped_pool.tile([P, SPAN_K], BF16, name="grouped", align_bytes=64)
             words = grouped_tiles[n][:].bitcast(F32).rearrange(
                 "p (j m u) -> p j m u", j=SPAN_PASSES, u=2
+            )
+            x_words = x_tiles[n][:].bitcast(F32).rearrange(
+                "p (j w u) -> p j u w", j=SPAN_PASSES, u=2
             )
             for half in range(SPAN_PASSES // 2):
                 bank = banks.tile([P, 2, 2, P], F32, name="x_bank", tag="bank")
@@ -157,13 +148,15 @@ def tile_attention_prop_pa_k_kernel(
                     for u in range(2):
                         nc.tensor.transpose(
                             out=bank[:, jj, u, :],
-                            in_=sorted_tiles[n][:, 2 * half + jj, u, :],
+                            in_=x_words[:, 2 * half + jj, u, :],
                             identity=ident_f32[:],
                         )
                 nc.scalar.copy(
                     out=words[:, 2 * half : 2 * half + 2],
                     in_=bank[:].rearrange("p j u m -> p j m u"),
                 )
+            if n + X_BUFS < len(order):
+                load_x_tile(n + X_BUFS)
 
         def quantise_x(n):
             codes = codes_pool.tile([P, SPAN_PASSES * P], U32, name="x_codes", align_bytes=64)
@@ -274,9 +267,7 @@ def tile_attention_prop_pa_k_kernel(
         nc.tensor.transpose(out=vec_bank[:], in_=vec_rows[:], identity=ident_bf16[:])
         nc.vector.tensor_copy(out=vec_cols[:], in_=vec_bank[:, 0 : 3 * FEAT_TILES])
 
-        for r in range(-2, len(runs) + 1):
-            for n in tiles_of(r + 2):
-                sort_words(n)
+        for r in range(-1, len(runs) + 1):
             for n in tiles_of(r + 1):
                 transpose_x(n)
             for a in closed_in(r - 1):

@@ -46,8 +46,8 @@ def tile_attention_prop_pa_k_kernel(
     for n, (a, s) in enumerate(order):
         if s not in spans_seen:
             spans_seen.append(s)
-            last_of_run = runs[n // RUN_TILES][-1]
-            weights_behind[last_of_run] = weights_behind.get(last_of_run, []) + [s]
+            last_of_next_run = runs[min(n // RUN_TILES + 1, len(runs) - 1)][-1]
+            weights_behind[last_of_next_run] = weights_behind.get(last_of_next_run, []) + [s]
 
     def tiles_of(r):
         return runs[r] if 0 <= r < len(runs) else []
@@ -58,6 +58,7 @@ def tile_attention_prop_pa_k_kernel(
     with ExitStack() as ctx:
         const = ctx.enter_context(tc.tile_pool(name="const", bufs=1))
         x_pool = ctx.enter_context(tc.tile_pool(name="x", bufs=X_BUFS))
+        sorted_pool = ctx.enter_context(tc.tile_pool(name="sorted", bufs=2 * RUN_TILES))
         grouped_pool = ctx.enter_context(tc.tile_pool(name="grouped", bufs=2 * RUN_TILES))
         codes_pool = ctx.enter_context(tc.tile_pool(name="codes", bufs=3 * RUN_TILES))
         tail = ctx.enter_context(tc.tile_pool(name="tail", bufs=2))
@@ -103,7 +104,7 @@ def tile_attention_prop_pa_k_kernel(
             sums.tile([P, FEATS], F32, name="acc%d" % a, tag="sum%d" % a) for a in range(ROW_TILES)
         ]
 
-        x_tiles, grouped_tiles, code_tiles, h1_tiles, h2_banks = {}, {}, {}, {}, {}
+        x_tiles, sorted_tiles, grouped_tiles, code_tiles, h1_tiles, h2_banks = {}, {}, {}, {}, {}, {}
 
         def load_scale_rows(plane, rows_per_quadrant, scale_rows):
             for quadrant in range(QUADRANTS):
@@ -121,6 +122,14 @@ def tile_attention_prop_pa_k_kernel(
             )
             for span in weights_behind.get(n, []):
                 load_span_weights(span)
+            if n == len(order) - 1:
+                load_scale_rows(
+                    w2_plane, 4, lambda quadrant: w2_scales[0, 4 * quadrant : 4 * quadrant + 4, :]
+                )
+                nc.sync.dma_start(
+                    out=w2_tile[:].bitcast(I32),
+                    in_=w2_words[0].rearrange("p n t -> p (n t)").bitcast(I32),
+                )
 
         def load_span_weights(s):
             groups = slice(s * SPAN_PASSES, (s + 1) * SPAN_PASSES)
@@ -134,13 +143,21 @@ def tile_attention_prop_pa_k_kernel(
                 in_=w1_words[groups].rearrange("g p n t -> p g (n t)").bitcast(I32),
             )
 
+        def sort_words(n):
+            sorted_tiles[n] = sorted_pool.tile([P, SPAN_PASSES, 2, P], F32, name="sorted_words")
+            nc.vector.tensor_copy(
+                out=sorted_tiles[n][:],
+                in_=x_tiles[n][:]
+                .bitcast(F32)
+                .rearrange("p (j w u) -> p j u w", j=SPAN_PASSES, u=2),
+            )
+            if n + X_BUFS < len(order):
+                load_x_tile(n + X_BUFS)
+
         def transpose_x(n):
             grouped_tiles[n] = grouped_pool.tile([P, SPAN_K], BF16, name="grouped", align_bytes=64)
             words = grouped_tiles[n][:].bitcast(F32).rearrange(
                 "p (j m u) -> p j m u", j=SPAN_PASSES, u=2
-            )
-            x_words = x_tiles[n][:].bitcast(F32).rearrange(
-                "p (j w u) -> p j u w", j=SPAN_PASSES, u=2
             )
             for half in range(SPAN_PASSES // 2):
                 bank = banks.tile([P, 2, 2, P], F32, name="x_bank", tag="bank")
@@ -148,15 +165,13 @@ def tile_attention_prop_pa_k_kernel(
                     for u in range(2):
                         nc.tensor.transpose(
                             out=bank[:, jj, u, :],
-                            in_=x_words[:, 2 * half + jj, u, :],
+                            in_=sorted_tiles[n][:, 2 * half + jj, u, :],
                             identity=ident_f32[:],
                         )
                 nc.scalar.copy(
                     out=words[:, 2 * half : 2 * half + 2],
                     in_=bank[:].rearrange("p j u m -> p j m u"),
                 )
-            if n + X_BUFS < len(order):
-                load_x_tile(n + X_BUFS)
 
         def quantise_x(n):
             codes = codes_pool.tile([P, SPAN_PASSES * P], U32, name="x_codes", align_bytes=64)
@@ -235,10 +250,16 @@ def tile_attention_prop_pa_k_kernel(
             for j in range(FEAT_TILES):
                 nc.vector.bn_stats(out=stats[:, j, a, :], in_=h2[:, j, a, :])
 
-        for plane in w1_planes + [w2_plane]:
-            nc.vector.memset(plane[:].bitcast(I32), 0)
         nc.vector.memset(b1_row[:], 0.0)
         nc.vector.memset(vec_rows[:], 0.0)
+        nc.scalar.dma_start(out=b1_row[0:1, :], in_=b1.rearrange("(o f) -> o f", o=1))
+        for i, vector in enumerate((b2, gamma, beta)):
+            nc.scalar.dma_start(
+                out=vec_rows[i * FEAT_TILES : (i + 1) * FEAT_TILES, :],
+                in_=vector.rearrange("(j p) -> j p", p=P),
+            )
+        for plane in w1_planes + [w2_plane]:
+            nc.vector.memset(plane[:].bitcast(I32), 0)
         nc.vector.memset(ones[:], 1.0)
         nc.vector.memset(one_col[:], 1.0)
         make_identity(nc, ident_f32[:])
@@ -246,18 +267,6 @@ def tile_attention_prop_pa_k_kernel(
 
         for n in range(X_BUFS):
             load_x_tile(n)
-        load_scale_rows(w2_plane, 4, lambda quadrant: w2_scales[0, 4 * quadrant : 4 * quadrant + 4, :])
-        nc.sync.dma_start(
-            out=w2_tile[:].bitcast(I32),
-            in_=w2_words[0].rearrange("p n t -> p (n t)").bitcast(I32),
-        )
-
-        nc.scalar.dma_start(out=b1_row[0:1, :], in_=b1.rearrange("(o f) -> o f", o=1))
-        for i, vector in enumerate((b2, gamma, beta)):
-            nc.scalar.dma_start(
-                out=vec_rows[i * FEAT_TILES : (i + 1) * FEAT_TILES, :],
-                in_=vector.rearrange("(j p) -> j p", p=P),
-            )
         nc.scalar.activation(out=root_col[:], in_=one_col[:], func=ACT.Sqrt)
 
         b1_bank = banks.tile([P, FEATS], F32, name="b1_bank", tag="bank")
@@ -267,7 +276,9 @@ def tile_attention_prop_pa_k_kernel(
         nc.tensor.transpose(out=vec_bank[:], in_=vec_rows[:], identity=ident_bf16[:])
         nc.vector.tensor_copy(out=vec_cols[:], in_=vec_bank[:, 0 : 3 * FEAT_TILES])
 
-        for r in range(-1, len(runs) + 1):
+        for r in range(-2, len(runs) + 2):
+            for n in tiles_of(r + 2):
+                sort_words(n)
             for n in tiles_of(r + 1):
                 transpose_x(n)
             for a in closed_in(r - 1):
@@ -278,11 +289,11 @@ def tile_attention_prop_pa_k_kernel(
                 quantise_hidden(a)
             for n in tiles_of(r):
                 first_layer_passes(n)
-            for a in closed_in(r - 1):
+            for a in closed_in(r - 2):
                 second_layer(a)
             for a in closed_in(r):
                 hidden_values(a)
-            for a in closed_in(r - 1):
+            for a in closed_in(r - 2):
                 second_layer_statistics(a)
 
         for j in range(FEAT_TILES):

@@ -21,7 +21,6 @@ FEAT_TILES = FEATS // P
 SPAN_PASSES = 4
 SPAN_K = SPAN_PASSES * K_PASS
 SPANS = K1 // SPAN_K
-LAST_SPANS = 2
 RUN_TILES = 2
 X_BUFS = 12
 QUADRANTS = 4
@@ -37,9 +36,7 @@ def tile_attention_prop_pa_k_kernel(
 ):
     nc = tc.nc
 
-    first_spans = SPANS - LAST_SPANS
-    order = [(a, s) for s in range(first_spans) for a in range(ROW_TILES)]
-    order += [(a, s) for a in range(ROW_TILES) for s in range(first_spans, SPANS)]
+    order = [(a, s) for s in range(SPANS) for a in range(ROW_TILES)]
     runs = [list(range(n, n + RUN_TILES)) for n in range(0, len(order), RUN_TILES)]
     weights_behind = {}
     spans_seen = []
@@ -62,6 +59,7 @@ def tile_attention_prop_pa_k_kernel(
         grouped_pool = ctx.enter_context(tc.tile_pool(name="grouped", bufs=2 * RUN_TILES))
         codes_pool = ctx.enter_context(tc.tile_pool(name="codes", bufs=3 * RUN_TILES))
         tail = ctx.enter_context(tc.tile_pool(name="tail", bufs=2))
+        last = ctx.enter_context(tc.tile_pool(name="last", bufs=FEAT_TILES))
         sums = ctx.enter_context(tc.psum_pool(name="sums", bufs=1))
         banks = ctx.enter_context(tc.psum_pool(name="banks", bufs=4))
         ctx.enter_context(tc.manual_schedule())
@@ -311,7 +309,7 @@ def tile_attention_prop_pa_k_kernel(
 
         out_by_row_tile = out.rearrange("(a m) f -> m a f", m=P)
         for j in range(FEAT_TILES):
-            normed = tail.tile([P, ROW_TILES, P], F32, name="normed")
+            normed = last.tile([P, ROW_TILES, P], F32, name="normed")
             nc.vector.tensor_scalar(
                 out=normed[:], in0=h2[:, j], scalar1=gain[:, j : j + 1], scalar2=shift[:, j : j + 1],
                 op0=ALU.mult, op1=ALU.add,
@@ -319,6 +317,6 @@ def tile_attention_prop_pa_k_kernel(
             out_bank = sums.tile([P, ROW_TILES, P], F32, name="out_bank", tag="sum%d" % j)
             for a in range(ROW_TILES):
                 nc.tensor.transpose(out=out_bank[:, a, :], in_=normed[:, a, :], identity=ident_f32[:])
-            out_rows = tail.tile([P, ROW_TILES, P], F32, name="out_rows")
+            out_rows = last.tile([P, ROW_TILES, P], F32, name="out_rows")
             nc.scalar.copy(out=out_rows[:], in_=out_bank[:])
             nc.sync.dma_start(out=out_by_row_tile[:, :, j * P : (j + 1) * P], in_=out_rows[:])

@@ -17,6 +17,7 @@ PACK = 4
 K_PASS = P * PACK
 ROWS, K1, FEATS = 512, 16384, 512
 ROW_TILES = ROWS // P
+HALF_ROWS = ROWS // 2
 FEAT_TILES = FEATS // P
 SPAN_PASSES = 4
 SPAN_K = SPAN_PASSES * K_PASS
@@ -89,8 +90,8 @@ def tile_attention_prop_pa_k_kernel(
         h1_grouped = const.tile([P, ROW_TILES, P, PACK], BF16, name="h1_grouped", align_bytes=64)
         h1_codes = const.tile([P, ROWS], U32, name="h1_codes", align_bytes=64)
         h1_scales = const.tile([P, ROWS], U8, name="h1_scales", align_bytes=64)
-        h2 = const.tile([P, FEAT_TILES, ROW_TILES, P], F32, name="h2")
-        stats = const.tile([P, FEAT_TILES, ROW_TILES, BN_STATS], F32, name="stats")
+        h2 = const.tile([P, FEAT_TILES, ROWS], F32, name="h2")
+        stats = const.tile([P, FEAT_TILES, 2, BN_STATS], F32, name="stats")
         mean_var = const.tile([P, FEAT_TILES, 2], F32, name="mean_var")
         var_eps = const.tile([P, FEAT_TILES], F32, name="var_eps")
         std = const.tile([P, FEAT_TILES], F32, name="std")
@@ -102,7 +103,7 @@ def tile_attention_prop_pa_k_kernel(
             sums.tile([P, FEATS], F32, name="acc%d" % a, tag="sum%d" % a) for a in range(ROW_TILES)
         ]
 
-        x_tiles, sorted_tiles, grouped_tiles, code_tiles, h1_tiles, h2_banks = {}, {}, {}, {}, {}, {}
+        x_tiles, sorted_tiles, grouped_tiles, code_tiles, h1_tiles = {}, {}, {}, {}, {}
 
         def load_scale_rows(plane, rows_per_quadrant, scale_rows):
             for quadrant in range(QUADRANTS):
@@ -197,7 +198,7 @@ def tile_attention_prop_pa_k_kernel(
         def hidden_values(a):
             biased = tail.tile([P, FEATS], F32, name="biased")
             nc.vector.tensor_tensor(out=biased[:], in0=acc[a][:], in1=b1_all[:], op=ALU.add)
-            h1_tiles[a] = tail.tile([P, FEATS], BF16, name="h1_rows")
+            h1_tiles[a] = last.tile([P, FEATS], BF16, name="h1_rows")
             nc.vector.scalar_tensor_tensor(
                 out=h1_tiles[a][:], in0=biased[:], scalar=SLOPE, in1=biased[:],
                 op0=ALU.mult, op1=ALU.max,
@@ -219,34 +220,27 @@ def tile_attention_prop_pa_k_kernel(
                 in_=h1_grouped[:, a].rearrange("p m t -> p (m t)"),
             )
 
-        def second_layer(a):
-            rows = slice(a * P, (a + 1) * P)
-            bank = sums.tile([P, FEAT_TILES, P], F32, name="h2_bank", tag="sum%d" % a)
-            biased = tail.tile([P, FEAT_TILES, P], F32, name="h2_biased")
-            for j in range(FEAT_TILES):
-                nc.tensor.matmul_mx(
-                    out=bank[:, j, :],
-                    lhsT=w2_tile[:, j * PACK * P : (j + 1) * PACK * P].bitcast(FP8X4),
-                    lhsT_scale=w2_plane[:, j * P : (j + 1) * P],
-                    rhs=h1_codes[:, rows].bitcast(FP8X4),
-                    rhs_scale=h1_scales[:, rows],
-                    start=True,
-                    stop=True,
-                )
-                nc.scalar.activation(
-                    out=biased[:, j, :], in_=bank[:, j, :], func=ACT.Identity,
-                    bias=b2_cols[:, j : j + 1], scale=1.0,
-                )
-            h2_banks[a] = biased
-
-        def second_layer_statistics(a):
-            biased = h2_banks[a]
+        def second_layer(half, j):
+            rows = slice(half * HALF_ROWS, (half + 1) * HALF_ROWS)
+            bank = banks.tile([P, HALF_ROWS], F32, name="h2_bank", tag="bank")
+            nc.tensor.matmul_mx(
+                out=bank[:],
+                lhsT=w2_tile[:, j * PACK * P : (j + 1) * PACK * P].bitcast(FP8X4),
+                lhsT_scale=w2_plane[:, j * P : (j + 1) * P],
+                rhs=h1_codes[:, rows].bitcast(FP8X4),
+                rhs_scale=h1_scales[:, rows],
+                start=True,
+                stop=True,
+            )
+            biased = tail.tile([P, HALF_ROWS], F32, name="h2_biased")
+            nc.scalar.activation(
+                out=biased[:], in_=bank[:], func=ACT.Identity, bias=b2_cols[:, j : j + 1], scale=1.0
+            )
             nc.vector.scalar_tensor_tensor(
-                out=h2[:, :, a, :], in0=biased[:], scalar=SLOPE, in1=biased[:],
+                out=h2[:, j, rows], in0=biased[:], scalar=SLOPE, in1=biased[:],
                 op0=ALU.mult, op1=ALU.max,
             )
-            for j in range(FEAT_TILES):
-                nc.vector.bn_stats(out=stats[:, j, a, :], in_=h2[:, j, a, :])
+            nc.vector.bn_stats(out=stats[:, j, half, :], in_=h2[:, j, rows])
 
         nc.vector.memset(b1_row[:], 0.0)
         nc.vector.memset(vec_rows[:], 0.0)
@@ -274,29 +268,28 @@ def tile_attention_prop_pa_k_kernel(
         nc.tensor.transpose(out=vec_bank[:], in_=vec_rows[:], identity=ident_bf16[:])
         nc.vector.tensor_copy(out=vec_cols[:], in_=vec_bank[:, 0 : 3 * FEAT_TILES])
 
-        for r in range(-2, len(runs) + 2):
+        for r in range(-2, len(runs)):
             for n in tiles_of(r + 2):
                 sort_words(n)
             for n in tiles_of(r + 1):
                 transpose_x(n)
-            for a in closed_in(r - 1):
-                transpose_hidden(a)
             for n in tiles_of(r + 1):
                 quantise_x(n)
-            for a in closed_in(r - 1):
-                quantise_hidden(a)
             for n in tiles_of(r):
                 first_layer_passes(n)
-            for a in closed_in(r - 2):
-                second_layer(a)
             for a in closed_in(r):
                 hidden_values(a)
-            for a in closed_in(r - 2):
-                second_layer_statistics(a)
+
+        for a in range(ROW_TILES):
+            transpose_hidden(a)
+            quantise_hidden(a)
+        for half in range(2):
+            for j in range(FEAT_TILES):
+                second_layer(half, j)
 
         for j in range(FEAT_TILES):
             nc.vector.bn_aggr(
-                out=mean_var[:, j, :], in_=stats[:, j].rearrange("p a c -> p (a c)")
+                out=mean_var[:, j, :], in_=stats[:, j].rearrange("p h c -> p (h c)")
             )
         nc.vector.tensor_scalar(
             out=var_eps[:], in0=mean_var[:, :, 1], scalar1=EPS, scalar2=None, op0=ALU.add
@@ -308,15 +301,22 @@ def tile_attention_prop_pa_k_kernel(
         nc.vector.tensor_tensor(out=shift[:], in0=beta_cols, in1=mean_gain[:], op=ALU.subtract)
 
         out_by_row_tile = out.rearrange("(a m) f -> m a f", m=P)
+        out_banks = []
         for j in range(FEAT_TILES):
             normed = last.tile([P, ROW_TILES, P], F32, name="normed")
             nc.vector.tensor_scalar(
-                out=normed[:], in0=h2[:, j], scalar1=gain[:, j : j + 1], scalar2=shift[:, j : j + 1],
+                out=normed[:].rearrange("p a m -> p (a m)"), in0=h2[:, j, :],
+                scalar1=gain[:, j : j + 1], scalar2=shift[:, j : j + 1],
                 op0=ALU.mult, op1=ALU.add,
             )
             out_bank = sums.tile([P, ROW_TILES, P], F32, name="out_bank", tag="sum%d" % j)
             for a in range(ROW_TILES):
                 nc.tensor.transpose(out=out_bank[:, a, :], in_=normed[:, a, :], identity=ident_f32[:])
+            out_banks.append(out_bank)
+        for j in range(FEAT_TILES):
             out_rows = last.tile([P, ROW_TILES, P], F32, name="out_rows")
-            nc.scalar.copy(out=out_rows[:], in_=out_bank[:])
+            if j % 2 == 0:
+                nc.scalar.copy(out=out_rows[:], in_=out_banks[j][:])
+            else:
+                nc.vector.tensor_copy(out=out_rows[:], in_=out_banks[j][:])
             nc.sync.dma_start(out=out_by_row_tile[:, :, j * P : (j + 1) * P], in_=out_rows[:])

@@ -195,6 +195,14 @@ def tile_attention_prop_pa_k_kernel(
                     stop=(s == SPANS - 1 and j == SPAN_PASSES - 1),
                 )
 
+        def spread_vectors():
+            b1_bank = banks.tile([P, FEATS], F32, name="b1_bank", tag="bank")
+            nc.tensor.matmul(out=b1_bank[:], lhsT=ones[:], rhs=b1_row[:], start=True, stop=True)
+            nc.scalar.copy(out=b1_all[:], in_=b1_bank[:])
+            vec_bank = banks.tile([P, P], BF16, name="vec_bank", tag="bank")
+            nc.tensor.transpose(out=vec_bank[:], in_=vec_rows[:], identity=ident_bf16[:])
+            nc.vector.tensor_copy(out=vec_cols[:], in_=vec_bank[:, 0 : 3 * FEAT_TILES])
+
         def hidden_values(a):
             biased = tail.tile([P, FEATS], F32, name="biased")
             nc.vector.tensor_tensor(out=biased[:], in0=acc[a][:], in1=b1_all[:], op=ALU.add)
@@ -261,13 +269,6 @@ def tile_attention_prop_pa_k_kernel(
             load_x_tile(n)
         nc.scalar.activation(out=root_col[:], in_=one_col[:], func=ACT.Sqrt)
 
-        b1_bank = banks.tile([P, FEATS], F32, name="b1_bank", tag="bank")
-        nc.tensor.matmul(out=b1_bank[:], lhsT=ones[:], rhs=b1_row[:], start=True, stop=True)
-        nc.scalar.copy(out=b1_all[:], in_=b1_bank[:])
-        vec_bank = banks.tile([P, P], BF16, name="vec_bank", tag="bank")
-        nc.tensor.transpose(out=vec_bank[:], in_=vec_rows[:], identity=ident_bf16[:])
-        nc.vector.tensor_copy(out=vec_cols[:], in_=vec_bank[:, 0 : 3 * FEAT_TILES])
-
         for r in range(-2, len(runs)):
             for n in tiles_of(r + 2):
                 sort_words(n)
@@ -277,6 +278,8 @@ def tile_attention_prop_pa_k_kernel(
                 quantise_x(n)
             for n in tiles_of(r):
                 first_layer_passes(n)
+            if r == 0:
+                spread_vectors()
             for a in closed_in(r):
                 hidden_values(a)
 

@@ -17,13 +17,14 @@ PACK = 4
 K_PASS = P * PACK
 ROWS, K1, FEATS = 512, 16384, 512
 ROW_TILES = ROWS // P
-HALF_ROWS = ROWS // 2
 FEAT_TILES = FEATS // P
 SPAN_PASSES = 4
 SPAN_K = SPAN_PASSES * K_PASS
 SPANS = K1 // SPAN_K
 RUN_TILES = 2
 X_BUFS = 12
+VECTORS_BEHIND = 11
+SPREAD_RUN = 8
 QUADRANTS = 4
 SLOPE = 0.01
 EPS = 1e-5
@@ -37,15 +38,17 @@ def tile_attention_prop_pa_k_kernel(
 ):
     nc = tc.nc
 
-    order = [(a, s) for s in range(SPANS) for a in range(ROW_TILES)]
+    early_spans, late_spans = range(SPANS - RUN_TILES), range(SPANS - RUN_TILES, SPANS)
+    order = [(a, s) for s in early_spans for a in range(ROW_TILES)]
+    order += [(a, s) for a in range(ROW_TILES) for s in late_spans]
     runs = [list(range(n, n + RUN_TILES)) for n in range(0, len(order), RUN_TILES)]
     weights_behind = {}
     spans_seen = []
     for n, (a, s) in enumerate(order):
         if s not in spans_seen:
             spans_seen.append(s)
-            last_of_next_run = runs[min(n // RUN_TILES + 1, len(runs) - 1)][-1]
-            weights_behind[last_of_next_run] = weights_behind.get(last_of_next_run, []) + [s]
+            run = 0 if n == 0 else min(n // RUN_TILES + 1, len(runs) - 1)
+            weights_behind[runs[run][-1]] = weights_behind.get(runs[run][-1], []) + [s]
 
     def tiles_of(r):
         return runs[r] if 0 <= r < len(runs) else []
@@ -91,9 +94,9 @@ def tile_attention_prop_pa_k_kernel(
         h1_codes = const.tile([P, ROWS], U32, name="h1_codes", align_bytes=64)
         h1_scales = const.tile([P, ROWS], U8, name="h1_scales", align_bytes=64)
         h2 = const.tile([P, FEAT_TILES, ROWS], F32, name="h2")
-        stats = const.tile([P, FEAT_TILES, 2, BN_STATS], F32, name="stats")
+        stats = const.tile([P, FEAT_TILES, ROW_TILES, BN_STATS], F32, name="stats")
         mean_var = const.tile([P, FEAT_TILES, 2], F32, name="mean_var")
-        var_eps = const.tile([P, FEAT_TILES], F32, name="var_eps")
+        mean_gamma = const.tile([P, FEAT_TILES], F32, name="mean_gamma")
         std = const.tile([P, FEAT_TILES], F32, name="std")
         rstd = const.tile([P, FEAT_TILES], F32, name="rstd")
         gain = const.tile([P, FEAT_TILES], F32, name="gain")
@@ -103,7 +106,8 @@ def tile_attention_prop_pa_k_kernel(
             sums.tile([P, FEATS], F32, name="acc%d" % a, tag="sum%d" % a) for a in range(ROW_TILES)
         ]
 
-        x_tiles, sorted_tiles, grouped_tiles, code_tiles, h1_tiles = {}, {}, {}, {}, {}
+        x_tiles, sorted_tiles, grouped_tiles, code_tiles = {}, {}, {}, {}
+        h1_tiles, biased_tiles = {}, {}
 
         def load_scale_rows(plane, rows_per_quadrant, scale_rows):
             for quadrant in range(QUADRANTS):
@@ -121,6 +125,8 @@ def tile_attention_prop_pa_k_kernel(
             )
             for span in weights_behind.get(n, []):
                 load_span_weights(span)
+            if n == VECTORS_BEHIND:
+                load_vectors()
             if n == len(order) - 1:
                 load_scale_rows(
                     w2_plane, 4, lambda quadrant: w2_scales[0, 4 * quadrant : 4 * quadrant + 4, :]
@@ -128,6 +134,14 @@ def tile_attention_prop_pa_k_kernel(
                 nc.sync.dma_start(
                     out=w2_tile[:].bitcast(I32),
                     in_=w2_words[0].rearrange("p n t -> p (n t)").bitcast(I32),
+                )
+
+        def load_vectors():
+            nc.sync.dma_start(out=b1_row[0:1, :], in_=b1.rearrange("(o f) -> o f", o=1))
+            for i, vector in enumerate((b2, gamma, beta)):
+                nc.sync.dma_start(
+                    out=vec_rows[i * FEAT_TILES : (i + 1) * FEAT_TILES, :],
+                    in_=vector.rearrange("(j p) -> j p", p=P),
                 )
 
         def load_span_weights(s):
@@ -228,38 +242,41 @@ def tile_attention_prop_pa_k_kernel(
                 in_=h1_grouped[:, a].rearrange("p m t -> p (m t)"),
             )
 
-        def second_layer(half, j):
-            rows = slice(half * HALF_ROWS, (half + 1) * HALF_ROWS)
-            bank = banks.tile([P, HALF_ROWS], F32, name="h2_bank", tag="bank")
-            nc.tensor.matmul_mx(
-                out=bank[:],
-                lhsT=w2_tile[:, j * PACK * P : (j + 1) * PACK * P].bitcast(FP8X4),
-                lhsT_scale=w2_plane[:, j * P : (j + 1) * P],
-                rhs=h1_codes[:, rows].bitcast(FP8X4),
-                rhs_scale=h1_scales[:, rows],
-                start=True,
-                stop=True,
-            )
-            biased = tail.tile([P, HALF_ROWS], F32, name="h2_biased")
-            nc.scalar.activation(
-                out=biased[:], in_=bank[:], func=ACT.Identity, bias=b2_cols[:, j : j + 1], scale=1.0
-            )
+        def second_layer(a):
+            rows = slice(a * P, (a + 1) * P)
+            bank = banks.tile([P, FEAT_TILES, P], F32, name="h2_bank", tag="bank")
+            biased_tiles[a] = tail.tile([P, FEAT_TILES, P], F32, name="h2_biased")
+            for j in range(FEAT_TILES):
+                nc.tensor.matmul_mx(
+                    out=bank[:, j, :],
+                    lhsT=w2_tile[:, j * PACK * P : (j + 1) * PACK * P].bitcast(FP8X4),
+                    lhsT_scale=w2_plane[:, j * P : (j + 1) * P],
+                    rhs=h1_codes[:, rows].bitcast(FP8X4),
+                    rhs_scale=h1_scales[:, rows],
+                    start=True,
+                    stop=True,
+                )
+            for j in range(FEAT_TILES):
+                nc.scalar.activation(
+                    out=biased_tiles[a][:, j, :], in_=bank[:, j, :], func=ACT.Identity,
+                    bias=b2_cols[:, j : j + 1], scale=1.0,
+                )
+
+        def output_values(a, tiles=slice(0, FEAT_TILES)):
+            biased = biased_tiles[a][:, tiles, :]
             nc.vector.scalar_tensor_tensor(
-                out=h2[:, j, rows], in0=biased[:], scalar=SLOPE, in1=biased[:],
+                out=h2[:, tiles, a * P : (a + 1) * P], in0=biased, scalar=SLOPE, in1=biased,
                 op0=ALU.mult, op1=ALU.max,
             )
-            nc.vector.bn_stats(out=stats[:, j, half, :], in_=h2[:, j, rows])
 
-        nc.vector.memset(b1_row[:], 0.0)
-        nc.vector.memset(vec_rows[:], 0.0)
-        nc.scalar.dma_start(out=b1_row[0:1, :], in_=b1.rearrange("(o f) -> o f", o=1))
-        for i, vector in enumerate((b2, gamma, beta)):
-            nc.scalar.dma_start(
-                out=vec_rows[i * FEAT_TILES : (i + 1) * FEAT_TILES, :],
-                in_=vector.rearrange("(j p) -> j p", p=P),
-            )
+        def row_tile_stats(a, tiles=range(FEAT_TILES)):
+            for j in tiles:
+                nc.vector.bn_stats(out=stats[:, j, a, :], in_=h2[:, j, a * P : (a + 1) * P])
+
         for plane in w1_planes + [w2_plane]:
             nc.vector.memset(plane[:].bitcast(I32), 0)
+        nc.vector.memset(b1_row[:], 0.0)
+        nc.vector.memset(vec_rows[:], 0.0)
         nc.vector.memset(ones[:], 1.0)
         nc.vector.memset(one_col[:], 1.0)
         make_identity(nc, ident_f32[:])
@@ -270,55 +287,90 @@ def tile_attention_prop_pa_k_kernel(
         nc.scalar.activation(out=root_col[:], in_=one_col[:], func=ACT.Sqrt)
 
         for r in range(-2, len(runs)):
-            for n in tiles_of(r + 2):
-                sort_words(n)
+            if r != -1:
+                for n in tiles_of(r + 2):
+                    sort_words(n)
             for n in tiles_of(r + 1):
                 transpose_x(n)
+            for a in closed_in(r - 2):
+                transpose_hidden(a)
             for n in tiles_of(r + 1):
                 quantise_x(n)
-            for n in tiles_of(r):
-                first_layer_passes(n)
-            if r == 0:
+            if r == -1:
+                for n in tiles_of(0):
+                    first_layer_passes(n)
+                for n in tiles_of(1):
+                    sort_words(n)
+            for a in closed_in(r - 2):
+                quantise_hidden(a)
+            for a in closed_in(r - 3):
+                second_layer(a)
+                output_values(a)
+                row_tile_stats(a)
+            if r > 0:
+                for n in tiles_of(r):
+                    first_layer_passes(n)
+            if r == SPREAD_RUN:
                 spread_vectors()
             for a in closed_in(r):
                 hidden_values(a)
 
-        for a in range(ROW_TILES):
-            transpose_hidden(a)
-            quantise_hidden(a)
-        for half in range(2):
-            for j in range(FEAT_TILES):
-                second_layer(half, j)
+        transpose_hidden(2)
+        second_layer(1)
+        quantise_hidden(2)
+        output_values(1)
+        transpose_hidden(3)
+        quantise_hidden(3)
+        second_layer(2)
+        row_tile_stats(1)
+        output_values(2)
+        second_layer(3)
+        row_tile_stats(2)
+        for j in range(FEAT_TILES + 1):
+            if j < FEAT_TILES:
+                output_values(3, slice(j, j + 1))
+            if j > 0:
+                row_tile_stats(3, [j - 1])
 
         for j in range(FEAT_TILES):
             nc.vector.bn_aggr(
                 out=mean_var[:, j, :], in_=stats[:, j].rearrange("p h c -> p (h c)")
             )
-        nc.vector.tensor_scalar(
-            out=var_eps[:], in0=mean_var[:, :, 1], scalar1=EPS, scalar2=None, op0=ALU.add
-        )
-        nc.scalar.activation(out=std[:], in_=var_eps[:], func=ACT.Sqrt)
+        nc.scalar.activation(out=std[:], in_=mean_var[:, :, 1], func=ACT.Sqrt, bias=EPS, scale=1.0)
+        nc.vector.tensor_tensor(out=mean_gamma[:], in0=mean_var[:, :, 0], in1=gamma_cols, op=ALU.mult)
         nc.vector.reciprocal(out=rstd[:], in_=std[:])
+        nc.vector.tensor_tensor(out=mean_gain[:], in0=mean_gamma[:], in1=rstd[:], op=ALU.mult)
         nc.vector.tensor_tensor(out=gain[:], in0=gamma_cols, in1=rstd[:], op=ALU.mult)
-        nc.vector.tensor_tensor(out=mean_gain[:], in0=mean_var[:, :, 0], in1=gain[:], op=ALU.mult)
         nc.vector.tensor_tensor(out=shift[:], in0=beta_cols, in1=mean_gain[:], op=ALU.subtract)
 
         out_by_row_tile = out.rearrange("(a m) f -> m a f", m=P)
-        out_banks = []
+        scalar_norms, scalar_copies = [3], [0, 3]
+        store_order = [0, 1, 3, 2]
+        normed_tiles, out_banks = {}, {}
         for j in range(FEAT_TILES):
             normed = last.tile([P, ROW_TILES, P], F32, name="normed")
-            nc.vector.tensor_scalar(
-                out=normed[:].rearrange("p a m -> p (a m)"), in0=h2[:, j, :],
-                scalar1=gain[:, j : j + 1], scalar2=shift[:, j : j + 1],
-                op0=ALU.mult, op1=ALU.add,
-            )
-            out_bank = sums.tile([P, ROW_TILES, P], F32, name="out_bank", tag="sum%d" % j)
+            flat = normed[:].rearrange("p a m -> p (a m)")
+            if j in scalar_norms:
+                nc.scalar.activation(
+                    out=flat, in_=h2[:, j, :], func=ACT.Identity,
+                    scale=gain[:, j : j + 1], bias=shift[:, j : j + 1],
+                )
+            else:
+                nc.vector.tensor_scalar(
+                    out=flat, in0=h2[:, j, :],
+                    scalar1=gain[:, j : j + 1], scalar2=shift[:, j : j + 1],
+                    op0=ALU.mult, op1=ALU.add,
+                )
+            normed_tiles[j] = normed
+        for j in store_order:
+            out_banks[j] = sums.tile([P, ROW_TILES, P], F32, name="out_bank", tag="sum%d" % j)
             for a in range(ROW_TILES):
-                nc.tensor.transpose(out=out_bank[:, a, :], in_=normed[:, a, :], identity=ident_f32[:])
-            out_banks.append(out_bank)
-        for j in range(FEAT_TILES):
+                nc.tensor.transpose(
+                    out=out_banks[j][:, a, :], in_=normed_tiles[j][:, a, :], identity=ident_f32[:]
+                )
+        for j in store_order:
             out_rows = last.tile([P, ROW_TILES, P], F32, name="out_rows")
-            if j % 2 == 0:
+            if j in scalar_copies:
                 nc.scalar.copy(out=out_rows[:], in_=out_banks[j][:])
             else:
                 nc.vector.tensor_copy(out=out_rows[:], in_=out_banks[j][:])

@@ -22,13 +22,17 @@ SPAN_PASSES = 4
 SPAN_K = SPAN_PASSES * K_PASS
 SPANS = K1 // SPAN_K
 RUN_TILES = 2
-X_BUFS = 12
-VECTORS_BEHIND = 11
+X_BUFS = 7
+VECTORS_BEHIND = 5
 SPREAD_RUN = 8
+WARM_FIRST, WARM_LATER = 8, 6
 QUADRANTS = 4
 SLOPE = 0.01
 EPS = 1e-5
 BN_STATS = 6
+
+LAST_TILES = [(0, SPANS - 2), (1, SPANS - 2), (0, SPANS - 1), (2, SPANS - 2),
+              (1, SPANS - 1), (3, SPANS - 2), (2, SPANS - 1), (3, SPANS - 1)]
 
 FLOPS = 2 * ROWS * K1 * FEATS + 2 * ROWS * FEATS * FEATS
 
@@ -38,17 +42,16 @@ def tile_attention_prop_pa_k_kernel(
 ):
     nc = tc.nc
 
-    early_spans, late_spans = range(SPANS - RUN_TILES), range(SPANS - RUN_TILES, SPANS)
-    order = [(a, s) for s in early_spans for a in range(ROW_TILES)]
-    order += [(a, s) for a in range(ROW_TILES) for s in late_spans]
+    order = [(a, s) for s in range(SPANS - 2) for a in range(ROW_TILES)]
+    order += LAST_TILES
     runs = [list(range(n, n + RUN_TILES)) for n in range(0, len(order), RUN_TILES)]
     weights_behind = {}
     spans_seen = []
     for n, (a, s) in enumerate(order):
         if s not in spans_seen:
             spans_seen.append(s)
-            run = 0 if n == 0 else min(n // RUN_TILES + 1, len(runs) - 1)
-            weights_behind[runs[run][-1]] = weights_behind.get(runs[run][-1], []) + [s]
+            run = 0 if n == 0 else n // RUN_TILES + 1
+            weights_behind[run] = weights_behind.get(run, []) + [s]
 
     def tiles_of(r):
         return runs[r] if 0 <= r < len(runs) else []
@@ -80,6 +83,7 @@ def tile_attention_prop_pa_k_kernel(
         w2_plane = const.tile([P, FEATS], U8, name="w2_plane", align_bytes=64)
         ident_f32 = const.tile([P, P], F32, name="ident_f32")
         ident_bf16 = const.tile([P, P], BF16, name="ident_bf16")
+        zeros = const.tile([P, FEATS], BF16, name="zeros")
         ones = const.tile([P, P], BF16, name="ones")
         b1_row = const.tile([P, FEATS], BF16, name="b1_row")
         b1_all = const.tile([P, FEATS], F32, name="b1_all")
@@ -106,7 +110,7 @@ def tile_attention_prop_pa_k_kernel(
             sums.tile([P, FEATS], F32, name="acc%d" % a, tag="sum%d" % a) for a in range(ROW_TILES)
         ]
 
-        x_tiles, sorted_tiles, grouped_tiles, code_tiles = {}, {}, {}, {}
+        x_runs, sorted_tiles, grouped_tiles, code_tiles = {}, {}, {}, {}
         h1_tiles, biased_tiles = {}, {}
 
         def load_scale_rows(plane, rows_per_quadrant, scale_rows):
@@ -117,17 +121,28 @@ def tile_attention_prop_pa_k_kernel(
                     in_=scale_rows(quadrant).bitcast(I32),
                 )
 
-        def load_x_tile(n):
-            a, s = order[n]
-            x_tiles[n] = x_pool.tile([P, SPAN_K], BF16, name="x_tile")
-            nc.sync.dma_start(
-                out=x_tiles[n][:], in_=x[a * P : (a + 1) * P, s * SPAN_K : (s + 1) * SPAN_K]
-            )
-            for span in weights_behind.get(n, []):
+        def load_run(r):
+            x_runs[r] = x_pool.tile([P, RUN_TILES, SPAN_K], BF16, name="x_run")
+            tiles = [order[n] for n in runs[r]]
+            (a, s), (a_next, s_next) = tiles
+            if s == s_next and a_next == a + 1:
+                nc.sync.dma_start(
+                    out=x_runs[r][:],
+                    in_=x[a * P : (a + RUN_TILES) * P, s * SPAN_K : (s + 1) * SPAN_K].rearrange(
+                        "(i m) k -> m i k", m=P
+                    ),
+                )
+            else:
+                for i, (a, s) in enumerate(tiles):
+                    nc.sync.dma_start(
+                        out=x_runs[r][:, i, :],
+                        in_=x[a * P : (a + 1) * P, s * SPAN_K : (s + 1) * SPAN_K],
+                    )
+            for span in weights_behind.get(r, []):
                 load_span_weights(span)
-            if n == VECTORS_BEHIND:
+            if r == VECTORS_BEHIND:
                 load_vectors()
-            if n == len(order) - 1:
+            if r == len(runs) - 1:
                 load_scale_rows(
                     w2_plane, 4, lambda quadrant: w2_scales[0, 4 * quadrant : 4 * quadrant + 4, :]
                 )
@@ -160,12 +175,13 @@ def tile_attention_prop_pa_k_kernel(
             sorted_tiles[n] = sorted_pool.tile([P, SPAN_PASSES, 2, P], F32, name="sorted_words")
             nc.vector.tensor_copy(
                 out=sorted_tiles[n][:],
-                in_=x_tiles[n][:]
+                in_=x_runs[n // RUN_TILES][:, n % RUN_TILES, :]
                 .bitcast(F32)
                 .rearrange("p (j w u) -> p j u w", j=SPAN_PASSES, u=2),
             )
-            if n + X_BUFS < len(order):
-                load_x_tile(n + X_BUFS)
+            r = n // RUN_TILES + X_BUFS
+            if n % RUN_TILES == RUN_TILES - 1 and r < len(runs):
+                load_run(r)
 
         def transpose_x(n):
             grouped_tiles[n] = grouped_pool.tile([P, SPAN_K], BF16, name="grouped", align_bytes=64)
@@ -209,13 +225,20 @@ def tile_attention_prop_pa_k_kernel(
                     stop=(s == SPANS - 1 and j == SPAN_PASSES - 1),
                 )
 
-        def spread_vectors():
+        def spread_b1():
             b1_bank = banks.tile([P, FEATS], F32, name="b1_bank", tag="bank")
             nc.tensor.matmul(out=b1_bank[:], lhsT=ones[:], rhs=b1_row[:], start=True, stop=True)
             nc.scalar.copy(out=b1_all[:], in_=b1_bank[:])
+        def spread_columns():
             vec_bank = banks.tile([P, P], BF16, name="vec_bank", tag="bank")
             nc.tensor.transpose(out=vec_bank[:], in_=vec_rows[:], identity=ident_bf16[:])
             nc.vector.tensor_copy(out=vec_cols[:], in_=vec_bank[:, 0 : 3 * FEAT_TILES])
+
+        def keep_busy(count):
+            for i in range(count):
+                nc.tensor.matmul(
+                    out=acc[ROW_TILES - 1][:], lhsT=zeros[:, 0:P], rhs=zeros[:], start=True, stop=True
+                )
 
         def hidden_values(a):
             biased = tail.tile([P, FEATS], F32, name="biased")
@@ -273,6 +296,7 @@ def tile_attention_prop_pa_k_kernel(
             for j in tiles:
                 nc.vector.bn_stats(out=stats[:, j, a, :], in_=h2[:, j, a * P : (a + 1) * P])
 
+        nc.vector.memset(zeros[:], 0.0)
         for plane in w1_planes + [w2_plane]:
             nc.vector.memset(plane[:].bitcast(I32), 0)
         nc.vector.memset(b1_row[:], 0.0)
@@ -282,21 +306,23 @@ def tile_attention_prop_pa_k_kernel(
         make_identity(nc, ident_f32[:])
         make_identity(nc, ident_bf16[:])
 
-        for n in range(X_BUFS):
-            load_x_tile(n)
+        for r in range(X_BUFS):
+            load_run(r)
+        keep_busy(WARM_FIRST)
         nc.scalar.activation(out=root_col[:], in_=one_col[:], func=ACT.Sqrt)
 
         for r in range(-2, len(runs)):
             if r != -1:
                 for n in tiles_of(r + 2):
                     sort_words(n)
-            for n in tiles_of(r + 1):
-                transpose_x(n)
             for a in closed_in(r - 2):
                 transpose_hidden(a)
             for n in tiles_of(r + 1):
+                transpose_x(n)
+            for n in tiles_of(r + 1):
                 quantise_x(n)
             if r == -1:
+                keep_busy(WARM_LATER)
                 for n in tiles_of(0):
                     first_layer_passes(n)
                 for n in tiles_of(1):
@@ -311,20 +337,27 @@ def tile_attention_prop_pa_k_kernel(
                 for n in tiles_of(r):
                     first_layer_passes(n)
             if r == SPREAD_RUN:
-                spread_vectors()
+                spread_b1()
+            if r == SPREAD_RUN + 1:
+                spread_columns()
             for a in closed_in(r):
                 hidden_values(a)
 
+        transpose_hidden(1)
+        second_layer(0)
+        quantise_hidden(1)
+        output_values(0)
+        row_tile_stats(0)
         transpose_hidden(2)
-        second_layer(1)
         quantise_hidden(2)
-        output_values(1)
+        second_layer(1)
         transpose_hidden(3)
         quantise_hidden(3)
         second_layer(2)
+        output_values(1)
         row_tile_stats(1)
-        output_values(2)
         second_layer(3)
+        output_values(2)
         row_tile_stats(2)
         for j in range(FEAT_TILES + 1):
             if j < FEAT_TILES:

@@ -17,6 +17,7 @@ PACK = 4
 K_PASS = P * PACK
 ROWS, K1, FEATS = 512, 16384, 512
 ROW_TILES = ROWS // P
+HALF_ROWS = ROWS // 2
 FEAT_TILES = FEATS // P
 SPAN_PASSES = 4
 SPAN_K = SPAN_PASSES * K_PASS
@@ -25,14 +26,13 @@ RUN_TILES = 2
 X_BUFS = 7
 VECTORS_BEHIND = 5
 SPREAD_RUN = 8
-WARM_FIRST, WARM_LATER = 8, 6
+WARM_FIRST, WARM_LATER, WARM_LAST = 8, 7, 10
 QUADRANTS = 4
 SLOPE = 0.01
 EPS = 1e-5
 BN_STATS = 6
 
-LAST_TILES = [(0, SPANS - 2), (1, SPANS - 2), (0, SPANS - 1), (2, SPANS - 2),
-              (1, SPANS - 1), (3, SPANS - 2), (2, SPANS - 1), (3, SPANS - 1)]
+LAST_TILES = [(a, s) for a in range(ROW_TILES) for s in (SPANS - 2, SPANS - 1)]
 
 FLOPS = 2 * ROWS * K1 * FEATS + 2 * ROWS * FEATS * FEATS
 
@@ -50,7 +50,7 @@ def tile_attention_prop_pa_k_kernel(
     for n, (a, s) in enumerate(order):
         if s not in spans_seen:
             spans_seen.append(s)
-            run = 0 if n == 0 else n // RUN_TILES + 1
+            run = n // RUN_TILES + 1
             weights_behind[run] = weights_behind.get(run, []) + [s]
 
     def tiles_of(r):
@@ -101,7 +101,6 @@ def tile_attention_prop_pa_k_kernel(
         stats = const.tile([P, FEAT_TILES, ROW_TILES, BN_STATS], F32, name="stats")
         mean_var = const.tile([P, FEAT_TILES, 2], F32, name="mean_var")
         mean_gamma = const.tile([P, FEAT_TILES], F32, name="mean_gamma")
-        std = const.tile([P, FEAT_TILES], F32, name="std")
         rstd = const.tile([P, FEAT_TILES], F32, name="rstd")
         gain = const.tile([P, FEAT_TILES], F32, name="gain")
         mean_gain = const.tile([P, FEAT_TILES], F32, name="mean_gain")
@@ -123,21 +122,25 @@ def tile_attention_prop_pa_k_kernel(
 
         def load_run(r):
             x_runs[r] = x_pool.tile([P, RUN_TILES, SPAN_K], BF16, name="x_run")
-            tiles = [order[n] for n in runs[r]]
-            (a, s), (a_next, s_next) = tiles
-            if s == s_next and a_next == a + 1:
+            (a, s), (a_last, s_last) = [order[n] for n in runs[r]]
+            if r == 0:
+                for i in range(RUN_TILES):
+                    nc.sync.dma_start(
+                        out=x_runs[r][:, i, :],
+                        in_=x[(a + i) * P : (a + i + 1) * P, s * SPAN_K : (s + 1) * SPAN_K],
+                    )
+            elif a == a_last:
+                nc.sync.dma_start(
+                    out=x_runs[r][:].rearrange("p i k -> p (i k)"),
+                    in_=x[a * P : (a + 1) * P, s * SPAN_K : (s_last + 1) * SPAN_K],
+                )
+            else:
                 nc.sync.dma_start(
                     out=x_runs[r][:],
-                    in_=x[a * P : (a + RUN_TILES) * P, s * SPAN_K : (s + 1) * SPAN_K].rearrange(
+                    in_=x[a * P : (a_last + 1) * P, s * SPAN_K : (s + 1) * SPAN_K].rearrange(
                         "(i m) k -> m i k", m=P
                     ),
                 )
-            else:
-                for i, (a, s) in enumerate(tiles):
-                    nc.sync.dma_start(
-                        out=x_runs[r][:, i, :],
-                        in_=x[a * P : (a + 1) * P, s * SPAN_K : (s + 1) * SPAN_K],
-                    )
             for span in weights_behind.get(r, []):
                 load_span_weights(span)
             if r == VECTORS_BEHIND:
@@ -234,10 +237,10 @@ def tile_attention_prop_pa_k_kernel(
             nc.tensor.transpose(out=vec_bank[:], in_=vec_rows[:], identity=ident_bf16[:])
             nc.vector.tensor_copy(out=vec_cols[:], in_=vec_bank[:, 0 : 3 * FEAT_TILES])
 
-        def keep_busy(count):
+        def keep_busy(a, count):
             for i in range(count):
                 nc.tensor.matmul(
-                    out=acc[ROW_TILES - 1][:], lhsT=zeros[:, 0:P], rhs=zeros[:], start=True, stop=True
+                    out=acc[a][:], lhsT=zeros[:, 0:P], rhs=zeros[:], start=True, stop=True
                 )
 
         def hidden_values(a):
@@ -308,34 +311,30 @@ def tile_attention_prop_pa_k_kernel(
 
         for r in range(X_BUFS):
             load_run(r)
-        keep_busy(WARM_FIRST)
-        nc.scalar.activation(out=root_col[:], in_=one_col[:], func=ACT.Sqrt)
+        keep_busy(ROW_TILES - 1, WARM_FIRST)
+        nc.scalar.activation(out=root_col[:], in_=one_col[:], func=ACT.Abs_reciprocal_sqrt)
 
         for r in range(-2, len(runs)):
-            if r != -1:
-                for n in tiles_of(r + 2):
-                    sort_words(n)
+            for n in tiles_of(r + 2):
+                sort_words(n)
             for a in closed_in(r - 2):
                 transpose_hidden(a)
             for n in tiles_of(r + 1):
                 transpose_x(n)
+            if r == -1:
+                keep_busy(ROW_TILES - 1, WARM_LATER)
             for n in tiles_of(r + 1):
                 quantise_x(n)
-            if r == -1:
-                keep_busy(WARM_LATER)
-                for n in tiles_of(0):
-                    first_layer_passes(n)
-                for n in tiles_of(1):
-                    sort_words(n)
             for a in closed_in(r - 2):
                 quantise_hidden(a)
             for a in closed_in(r - 3):
                 second_layer(a)
                 output_values(a)
                 row_tile_stats(a)
-            if r > 0:
-                for n in tiles_of(r):
-                    first_layer_passes(n)
+            for n in tiles_of(r):
+                first_layer_passes(n)
+                if n == len(order) - RUN_TILES:
+                    second_layer(1)
             if r == SPREAD_RUN:
                 spread_b1()
             if r == SPREAD_RUN + 1:
@@ -343,22 +342,17 @@ def tile_attention_prop_pa_k_kernel(
             for a in closed_in(r):
                 hidden_values(a)
 
-        transpose_hidden(1)
-        second_layer(0)
-        quantise_hidden(1)
-        output_values(0)
-        row_tile_stats(0)
         transpose_hidden(2)
         quantise_hidden(2)
-        second_layer(1)
-        transpose_hidden(3)
-        quantise_hidden(3)
-        second_layer(2)
         output_values(1)
         row_tile_stats(1)
-        second_layer(3)
+        transpose_hidden(3)
+        second_layer(2)
+        quantise_hidden(3)
         output_values(2)
+        second_layer(3)
         row_tile_stats(2)
+        keep_busy(0, WARM_LAST)
         for j in range(FEAT_TILES + 1):
             if j < FEAT_TILES:
                 output_values(3, slice(j, j + 1))
@@ -369,42 +363,36 @@ def tile_attention_prop_pa_k_kernel(
             nc.vector.bn_aggr(
                 out=mean_var[:, j, :], in_=stats[:, j].rearrange("p h c -> p (h c)")
             )
-        nc.scalar.activation(out=std[:], in_=mean_var[:, :, 1], func=ACT.Sqrt, bias=EPS, scale=1.0)
+        nc.scalar.activation(
+            out=rstd[:], in_=mean_var[:, :, 1], func=ACT.Abs_reciprocal_sqrt, bias=EPS, scale=1.0
+        )
         nc.vector.tensor_tensor(out=mean_gamma[:], in0=mean_var[:, :, 0], in1=gamma_cols, op=ALU.mult)
-        nc.vector.reciprocal(out=rstd[:], in_=std[:])
         nc.vector.tensor_tensor(out=mean_gain[:], in0=mean_gamma[:], in1=rstd[:], op=ALU.mult)
         nc.vector.tensor_tensor(out=gain[:], in0=gamma_cols, in1=rstd[:], op=ALU.mult)
         nc.vector.tensor_tensor(out=shift[:], in0=beta_cols, in1=mean_gain[:], op=ALU.subtract)
 
-        out_by_row_tile = out.rearrange("(a m) f -> m a f", m=P)
-        scalar_norms, scalar_copies = [3], [0, 3]
-        store_order = [0, 1, 3, 2]
-        normed_tiles, out_banks = {}, {}
-        for j in range(FEAT_TILES):
-            normed = last.tile([P, ROW_TILES, P], F32, name="normed")
-            flat = normed[:].rearrange("p a m -> p (a m)")
-            if j in scalar_norms:
-                nc.scalar.activation(
-                    out=flat, in_=h2[:, j, :], func=ACT.Identity,
-                    scale=gain[:, j : j + 1], bias=shift[:, j : j + 1],
-                )
-            else:
-                nc.vector.tensor_scalar(
-                    out=flat, in0=h2[:, j, :],
-                    scalar1=gain[:, j : j + 1], scalar2=shift[:, j : j + 1],
-                    op0=ALU.mult, op1=ALU.add,
-                )
-            normed_tiles[j] = normed
-        for j in store_order:
-            out_banks[j] = sums.tile([P, ROW_TILES, P], F32, name="out_bank", tag="sum%d" % j)
-            for a in range(ROW_TILES):
+        normed = const.tile([P, FEAT_TILES, ROWS], F32, name="normed")
+        for half in range(2):
+            rows = slice(half * HALF_ROWS, (half + 1) * HALF_ROWS)
+            for j in range(FEAT_TILES):
+                if j == FEAT_TILES - 1:
+                    nc.scalar.activation(
+                        out=normed[:, j, rows], in_=h2[:, j, rows], func=ACT.Identity,
+                        scale=gain[:, j : j + 1], bias=shift[:, j : j + 1],
+                    )
+                else:
+                    nc.vector.tensor_scalar(
+                        out=normed[:, j, rows], in0=h2[:, j, rows],
+                        scalar1=gain[:, j : j + 1], scalar2=shift[:, j : j + 1],
+                        op0=ALU.mult, op1=ALU.add,
+                    )
+        for a in range(ROW_TILES):
+            out_bank = sums.tile([P, FEAT_TILES, P], F32, name="out_bank", tag="sum%d" % a)
+            for j in range(FEAT_TILES):
                 nc.tensor.transpose(
-                    out=out_banks[j][:, a, :], in_=normed_tiles[j][:, a, :], identity=ident_f32[:]
+                    out=out_bank[:, j, :], in_=normed[:, j, a * P : (a + 1) * P], identity=ident_f32[:]
                 )
-        for j in store_order:
-            out_rows = last.tile([P, ROW_TILES, P], F32, name="out_rows")
-            if j in scalar_copies:
-                nc.scalar.copy(out=out_rows[:], in_=out_banks[j][:])
-            else:
-                nc.vector.tensor_copy(out=out_rows[:], in_=out_banks[j][:])
-            nc.sync.dma_start(out=out_by_row_tile[:, :, j * P : (j + 1) * P], in_=out_rows[:])
+            out_rows = last.tile([P, FEATS], F32, name="out_rows")
+            copy = nc.vector.tensor_copy if a % 2 else nc.scalar.copy
+            copy(out=out_rows[:], in_=out_bank[:].rearrange("p j f -> p (j f)"))
+            nc.sync.dma_start(out=out[a * P : (a + 1) * P, :], in_=out_rows[:])

@@ -17,8 +17,8 @@ PACK = 4
 K_PASS = P * PACK
 ROWS, K1, FEATS = 512, 16384, 512
 ROW_TILES = ROWS // P
-HALF_ROWS = ROWS // 2
 FEAT_TILES = FEATS // P
+HALF_FEATS = FEATS // 2
 SPAN_PASSES = 4
 SPAN_K = SPAN_PASSES * K_PASS
 SPANS = K1 // SPAN_K
@@ -26,7 +26,7 @@ RUN_TILES = 2
 X_BUFS = 7
 VECTORS_BEHIND = 5
 SPREAD_RUN = 8
-WARM_FIRST, WARM_LATER, WARM_LAST = 8, 7, 10
+WARM_FIRST, WARM_LATER, WARM_LAST = 8, 7, 14
 QUADRANTS = 4
 SLOPE = 0.01
 EPS = 1e-5
@@ -72,15 +72,15 @@ def tile_attention_prop_pa_k_kernel(
         ctx.enter_context(tc.manual_schedule())
 
         w1_tiles = [
-            const.tile([P, SPAN_PASSES, PACK * FEATS], U8, name="w1_span%d" % s, align_bytes=64)
+            const.tile([P, SPAN_PASSES, PACK * FEATS], U8, name="w1_span%d" % s, align_bytes=256)
             for s in range(SPANS)
         ]
         w1_planes = [
-            const.tile([P, FEATS], U8, name="w1_planes%d" % s, align_bytes=64)
+            const.tile([P, FEATS], U8, name="w1_planes%d" % s, align_bytes=256)
             for s in range(SPANS)
         ]
-        w2_tile = const.tile([P, PACK * FEATS], U8, name="w2_tile", align_bytes=64)
-        w2_plane = const.tile([P, FEATS], U8, name="w2_plane", align_bytes=64)
+        w2_tile = const.tile([P, PACK * FEATS], U8, name="w2_tile", align_bytes=256)
+        w2_plane = const.tile([P, FEATS], U8, name="w2_plane", align_bytes=256)
         ident_f32 = const.tile([P, P], F32, name="ident_f32")
         ident_bf16 = const.tile([P, P], BF16, name="ident_bf16")
         zeros = const.tile([P, FEATS], BF16, name="zeros")
@@ -94,9 +94,9 @@ def tile_attention_prop_pa_k_kernel(
         beta_cols = vec_cols[:, 2 * FEAT_TILES : 3 * FEAT_TILES]
         one_col = const.tile([P, 1], F32, name="one_col")
         root_col = const.tile([P, 1], F32, name="root_col")
-        h1_grouped = const.tile([P, ROW_TILES, P, PACK], BF16, name="h1_grouped", align_bytes=64)
-        h1_codes = const.tile([P, ROWS], U32, name="h1_codes", align_bytes=64)
-        h1_scales = const.tile([P, ROWS], U8, name="h1_scales", align_bytes=64)
+        h1_grouped = const.tile([P, ROW_TILES, P, PACK], BF16, name="h1_grouped", align_bytes=256)
+        h1_codes = const.tile([P, ROWS], U32, name="h1_codes", align_bytes=256)
+        h1_scales = const.tile([P, ROWS], U8, name="h1_scales", align_bytes=256)
         h2 = const.tile([P, FEAT_TILES, ROWS], F32, name="h2")
         stats = const.tile([P, FEAT_TILES, ROW_TILES, BN_STATS], F32, name="stats")
         mean_var = const.tile([P, FEAT_TILES, 2], F32, name="mean_var")
@@ -187,7 +187,7 @@ def tile_attention_prop_pa_k_kernel(
                 load_run(r)
 
         def transpose_x(n):
-            grouped_tiles[n] = grouped_pool.tile([P, SPAN_K], BF16, name="grouped", align_bytes=64)
+            grouped_tiles[n] = grouped_pool.tile([P, SPAN_K], BF16, name="grouped", align_bytes=256)
             words = grouped_tiles[n][:].bitcast(F32).rearrange(
                 "p (j m u) -> p j m u", j=SPAN_PASSES, u=2
             )
@@ -206,8 +206,8 @@ def tile_attention_prop_pa_k_kernel(
                 )
 
         def quantise_x(n):
-            codes = codes_pool.tile([P, SPAN_PASSES * P], U32, name="x_codes", align_bytes=64)
-            scales = codes_pool.tile([P, SPAN_PASSES * P], U8, name="x_scales", align_bytes=64)
+            codes = codes_pool.tile([P, SPAN_PASSES * P], U32, name="x_codes", align_bytes=256)
+            scales = codes_pool.tile([P, SPAN_PASSES * P], U8, name="x_scales", align_bytes=256)
             nc.vector.quantize_mx(
                 out=codes[:].bitcast(FP8X4), scales=scales[:], in_=grouped_tiles[n][:]
             )
@@ -372,8 +372,8 @@ def tile_attention_prop_pa_k_kernel(
         nc.vector.tensor_tensor(out=shift[:], in0=beta_cols, in1=mean_gain[:], op=ALU.subtract)
 
         normed = const.tile([P, FEAT_TILES, ROWS], F32, name="normed")
-        for half in range(2):
-            rows = slice(half * HALF_ROWS, (half + 1) * HALF_ROWS)
+        for a in range(ROW_TILES):
+            rows = slice(a * P, (a + 1) * P)
             for j in range(FEAT_TILES):
                 if j == FEAT_TILES - 1:
                     nc.scalar.activation(
@@ -387,12 +387,20 @@ def tile_attention_prop_pa_k_kernel(
                         op0=ALU.mult, op1=ALU.add,
                     )
         for a in range(ROW_TILES):
-            out_bank = sums.tile([P, FEAT_TILES, P], F32, name="out_bank", tag="sum%d" % a)
-            for j in range(FEAT_TILES):
-                nc.tensor.transpose(
-                    out=out_bank[:, j, :], in_=normed[:, j, a * P : (a + 1) * P], identity=ident_f32[:]
-                )
-            out_rows = last.tile([P, FEATS], F32, name="out_rows")
-            copy = nc.vector.tensor_copy if a % 2 else nc.scalar.copy
-            copy(out=out_rows[:], in_=out_bank[:].rearrange("p j f -> p (j f)"))
-            nc.sync.dma_start(out=out[a * P : (a + 1) * P, :], in_=out_rows[:])
+            out_rows = last.tile([P, 2, HALF_FEATS], F32, name="out_rows")
+            for half in range(2):
+                if half:
+                    out_bank = banks.tile([P, FEAT_TILES // 2, P], F32, name="out_bank_b", tag="bank")
+                else:
+                    out_bank = sums.tile([P, FEAT_TILES // 2, P], F32, name="out_bank_a", tag="sum%d" % a)
+                for i in range(FEAT_TILES // 2):
+                    nc.tensor.transpose(
+                        out=out_bank[:, i, :],
+                        in_=normed[:, half * FEAT_TILES // 2 + i, a * P : (a + 1) * P],
+                        identity=ident_f32[:],
+                    )
+                copy = nc.vector.tensor_copy if half else nc.scalar.copy
+                copy(out=out_rows[:, half, :], in_=out_bank[:].rearrange("p j f -> p (j f)"))
+            nc.sync.dma_start(
+                out=out[a * P : (a + 1) * P, :], in_=out_rows[:].rearrange("p h f -> p (h f)")
+            )

@@ -20,19 +20,21 @@ ROW_TILES = ROWS // P
 FEAT_TILES = FEATS // P
 HALF_FEATS = FEATS // 2
 SPAN_PASSES = 4
-SPAN_K = SPAN_PASSES * K_PASS
-SPANS = K1 // SPAN_K
-RUN_TILES = 2
+GROUPS = K1 // K_PASS
+SPANS = GROUPS // SPAN_PASSES
+UNIT_K = SPAN_PASSES * K_PASS
+WIDE_SPANS = 2
+LAST_SPANS = 2
+RUN_UNITS = 2
 X_BUFS = 7
 VECTORS_BEHIND = 5
 SPREAD_RUN = 8
-WARM_FIRST, WARM_LATER, WARM_LAST = 8, 7, 14
+WARM_BETWEEN = 3
+WARM_FIRST, WARM_LATER, WARM_LAST = 8, 4, 14
 QUADRANTS = 4
 SLOPE = 0.01
 EPS = 1e-5
 BN_STATS = 6
-
-LAST_TILES = [(a, s) for a in range(ROW_TILES) for s in (SPANS - 2, SPANS - 1)]
 
 FLOPS = 2 * ROWS * K1 * FEATS + 2 * ROWS * FEATS * FEATS
 
@@ -42,29 +44,40 @@ def tile_attention_prop_pa_k_kernel(
 ):
     nc = tc.nc
 
-    order = [(a, s) for s in range(SPANS - 2) for a in range(ROW_TILES)]
-    order += LAST_TILES
-    runs = [list(range(n, n + RUN_TILES)) for n in range(0, len(order), RUN_TILES)]
-    weights_behind = {}
-    spans_seen = []
-    for n, (a, s) in enumerate(order):
-        if s not in spans_seen:
-            spans_seen.append(s)
-            run = n // RUN_TILES + 1
-            weights_behind[run] = weights_behind.get(run, []) + [s]
+    def of_span(a, s):
+        return [(a, s * SPAN_PASSES + i) for i in range(SPAN_PASSES)]
 
-    def tiles_of(r):
+    order = [
+        [(a + i, g + j) for i in range(2) for j in range(2)]
+        for g in range(0, WIDE_SPANS * SPAN_PASSES, 2)
+        for a in range(0, ROW_TILES, 2)
+    ]
+    order += [of_span(a, s) for s in range(WIDE_SPANS, SPANS - LAST_SPANS) for a in range(ROW_TILES)]
+    order += [of_span(a, s) for a in range(ROW_TILES) for s in range(SPANS - LAST_SPANS, SPANS)]
+    runs = [list(range(n, n + RUN_UNITS)) for n in range(0, len(order), RUN_UNITS)]
+
+    weight_loads = [range(g, g + 2) for g in range(0, WIDE_SPANS * SPAN_PASSES, 2)]
+    weight_loads += [
+        range(s * SPAN_PASSES, (s + 1) * SPAN_PASSES) for s in range(WIDE_SPANS, SPANS)
+    ]
+    weights_behind = {}
+    for groups in weight_loads:
+        needed = min(n for n, unit in enumerate(order) if (unit[0][0], groups[0]) in unit)
+        run = needed // RUN_UNITS + 1
+        weights_behind[run] = weights_behind.get(run, []) + [groups]
+
+    def units_of(r):
         return runs[r] if 0 <= r < len(runs) else []
 
     def closed_in(r):
-        return [order[n][0] for n in tiles_of(r) if order[n][1] == SPANS - 1]
+        return [a for n in units_of(r) for a, g in order[n] if g == GROUPS - 1]
 
     with ExitStack() as ctx:
         const = ctx.enter_context(tc.tile_pool(name="const", bufs=1))
         x_pool = ctx.enter_context(tc.tile_pool(name="x", bufs=X_BUFS))
-        sorted_pool = ctx.enter_context(tc.tile_pool(name="sorted", bufs=2 * RUN_TILES))
-        grouped_pool = ctx.enter_context(tc.tile_pool(name="grouped", bufs=2 * RUN_TILES))
-        codes_pool = ctx.enter_context(tc.tile_pool(name="codes", bufs=3 * RUN_TILES))
+        sorted_pool = ctx.enter_context(tc.tile_pool(name="sorted", bufs=2 * RUN_UNITS))
+        grouped_pool = ctx.enter_context(tc.tile_pool(name="grouped", bufs=2 * RUN_UNITS))
+        codes_pool = ctx.enter_context(tc.tile_pool(name="codes", bufs=3 * RUN_UNITS))
         tail = ctx.enter_context(tc.tile_pool(name="tail", bufs=2))
         last = ctx.enter_context(tc.tile_pool(name="last", bufs=FEAT_TILES))
         sums = ctx.enter_context(tc.psum_pool(name="sums", bufs=1))
@@ -81,7 +94,7 @@ def tile_attention_prop_pa_k_kernel(
         ]
         w2_tile = const.tile([P, PACK * FEATS], U8, name="w2_tile", align_bytes=256)
         w2_plane = const.tile([P, FEATS], U8, name="w2_plane", align_bytes=256)
-        ident_f32 = const.tile([P, P], F32, name="ident_f32")
+        ident_f32 = const.tile([P, P], F32, name="ident_f32", align_bytes=256)
         ident_bf16 = const.tile([P, P], BF16, name="ident_bf16")
         zeros = const.tile([P, FEATS], BF16, name="zeros")
         ones = const.tile([P, P], BF16, name="ones")
@@ -120,29 +133,30 @@ def tile_attention_prop_pa_k_kernel(
                     in_=scale_rows(quadrant).bitcast(I32),
                 )
 
-        def load_run(r):
-            x_runs[r] = x_pool.tile([P, RUN_TILES, SPAN_K], BF16, name="x_run")
-            (a, s), (a_last, s_last) = [order[n] for n in runs[r]]
-            if r == 0:
-                for i in range(RUN_TILES):
-                    nc.sync.dma_start(
-                        out=x_runs[r][:, i, :],
-                        in_=x[(a + i) * P : (a + i + 1) * P, s * SPAN_K : (s + 1) * SPAN_K],
-                    )
-            elif a == a_last:
-                nc.sync.dma_start(
-                    out=x_runs[r][:].rearrange("p i k -> p (i k)"),
-                    in_=x[a * P : (a + 1) * P, s * SPAN_K : (s_last + 1) * SPAN_K],
-                )
+        def load_x(tile, units):
+            pairs = [pair for n in units for pair in order[n]]
+            first, last_row = pairs[0][0], pairs[-1][0]
+            k = slice(pairs[0][1] * K_PASS, (pairs[-1][1] + 1) * K_PASS)
+            if first == last_row:
+                nc.sync.dma_start(out=tile, in_=x[first * P : (first + 1) * P, k])
             else:
                 nc.sync.dma_start(
-                    out=x_runs[r][:],
-                    in_=x[a * P : (a_last + 1) * P, s * SPAN_K : (s + 1) * SPAN_K].rearrange(
-                        "(i m) k -> m i k", m=P
-                    ),
+                    out=tile.rearrange("p (a k) -> p a k", a=last_row - first + 1),
+                    in_=x[first * P : (last_row + 1) * P, k].rearrange("(a m) k -> m a k", m=P),
                 )
-            for span in weights_behind.get(r, []):
-                load_span_weights(span)
+
+        def load_run(r):
+            x_runs[r] = x_pool.tile([P, RUN_UNITS * UNIT_K], BF16, name="x_run")
+            one, other = [order[n] for n in runs[r]]
+            same_rows = one[0][0] == other[-1][0]
+            same_groups = one[0][1] == other[0][1]
+            if r > 0 and (same_rows or same_groups):
+                load_x(x_runs[r][:], runs[r])
+            else:
+                for i, n in enumerate(runs[r]):
+                    load_x(x_runs[r][:, i * UNIT_K : (i + 1) * UNIT_K], [n])
+            for groups in weights_behind.get(r, []):
+                load_weights(groups)
             if r == VECTORS_BEHIND:
                 load_vectors()
             if r == len(runs) - 1:
@@ -162,32 +176,38 @@ def tile_attention_prop_pa_k_kernel(
                     in_=vector.rearrange("(j p) -> j p", p=P),
                 )
 
-        def load_span_weights(s):
-            groups = slice(s * SPAN_PASSES, (s + 1) * SPAN_PASSES)
-            load_scale_rows(
-                w1_planes[s],
-                4 * SPAN_PASSES,
-                lambda quadrant: w1_scales[groups, 4 * quadrant : 4 * quadrant + 4, :],
-            )
+        def load_weights(groups):
+            s, first = divmod(groups[0], SPAN_PASSES)
+            if first == 0:
+                span = slice(s * SPAN_PASSES, (s + 1) * SPAN_PASSES)
+                load_scale_rows(
+                    w1_planes[s],
+                    4 * SPAN_PASSES,
+                    lambda quadrant: w1_scales[span, 4 * quadrant : 4 * quadrant + 4, :],
+                )
             nc.sync.dma_start(
-                out=w1_tiles[s][:].bitcast(I32),
-                in_=w1_words[groups].rearrange("g p n t -> p g (n t)").bitcast(I32),
+                out=w1_tiles[s][:, first : first + len(groups), :].bitcast(I32),
+                in_=w1_words[groups[0] : groups[-1] + 1]
+                .rearrange("g p n t -> p g (n t)")
+                .bitcast(I32),
             )
 
         def sort_words(n):
-            sorted_tiles[n] = sorted_pool.tile([P, SPAN_PASSES, 2, P], F32, name="sorted_words")
+            sorted_tiles[n] = sorted_pool.tile(
+                [P, SPAN_PASSES, 2, P], F32, name="sorted_words", align_bytes=256
+            )
             nc.vector.tensor_copy(
                 out=sorted_tiles[n][:],
-                in_=x_runs[n // RUN_TILES][:, n % RUN_TILES, :]
+                in_=x_runs[n // RUN_UNITS][:, (n % RUN_UNITS) * UNIT_K : (n % RUN_UNITS + 1) * UNIT_K]
                 .bitcast(F32)
                 .rearrange("p (j w u) -> p j u w", j=SPAN_PASSES, u=2),
             )
-            r = n // RUN_TILES + X_BUFS
-            if n % RUN_TILES == RUN_TILES - 1 and r < len(runs):
+            r = n // RUN_UNITS + X_BUFS
+            if n % RUN_UNITS == RUN_UNITS - 1 and r < len(runs):
                 load_run(r)
 
         def transpose_x(n):
-            grouped_tiles[n] = grouped_pool.tile([P, SPAN_K], BF16, name="grouped", align_bytes=256)
+            grouped_tiles[n] = grouped_pool.tile([P, UNIT_K], BF16, name="grouped", align_bytes=256)
             words = grouped_tiles[n][:].bitcast(F32).rearrange(
                 "p (j m u) -> p j m u", j=SPAN_PASSES, u=2
             )
@@ -214,18 +234,18 @@ def tile_attention_prop_pa_k_kernel(
             code_tiles[n] = (codes, scales)
 
         def first_layer_passes(n):
-            a, s = order[n]
             codes, scales = code_tiles[n]
-            for j in range(SPAN_PASSES):
-                rows = slice(j * P, (j + 1) * P)
+            for i, (a, g) in enumerate(order[n]):
+                rows = slice(i * P, (i + 1) * P)
+                s, j = divmod(g, SPAN_PASSES)
                 nc.tensor.matmul_mx(
                     out=acc[a][:],
                     lhsT=codes[:, rows].bitcast(FP8X4),
                     lhsT_scale=scales[:, rows],
                     rhs=w1_tiles[s][:, j, :].bitcast(FP8X4),
                     rhs_scale=w1_planes[s][4 * j : P, :],
-                    start=(s == 0 and j == 0),
-                    stop=(s == SPANS - 1 and j == SPAN_PASSES - 1),
+                    start=(g == 0),
+                    stop=(g == GROUPS - 1),
                 )
 
         def spread_b1():
@@ -315,15 +335,15 @@ def tile_attention_prop_pa_k_kernel(
         nc.scalar.activation(out=root_col[:], in_=one_col[:], func=ACT.Abs_reciprocal_sqrt)
 
         for r in range(-2, len(runs)):
-            for n in tiles_of(r + 2):
+            for n in units_of(r + 2):
                 sort_words(n)
             for a in closed_in(r - 2):
                 transpose_hidden(a)
-            for n in tiles_of(r + 1):
+            for n in units_of(r + 1):
                 transpose_x(n)
             if r == -1:
                 keep_busy(ROW_TILES - 1, WARM_LATER)
-            for n in tiles_of(r + 1):
+            for n in units_of(r + 1):
                 quantise_x(n)
             for a in closed_in(r - 2):
                 quantise_hidden(a)
@@ -331,9 +351,9 @@ def tile_attention_prop_pa_k_kernel(
                 second_layer(a)
                 output_values(a)
                 row_tile_stats(a)
-            for n in tiles_of(r):
+            for n in units_of(r):
                 first_layer_passes(n)
-                if n == len(order) - RUN_TILES:
+                if n == len(order) - RUN_UNITS:
                     second_layer(1)
             if r == SPREAD_RUN:
                 spread_b1()
@@ -343,11 +363,13 @@ def tile_attention_prop_pa_k_kernel(
                 hidden_values(a)
 
         transpose_hidden(2)
+        keep_busy(0, WARM_BETWEEN)
         quantise_hidden(2)
         output_values(1)
         row_tile_stats(1)
         transpose_hidden(3)
         second_layer(2)
+        keep_busy(0, WARM_BETWEEN)
         quantise_hidden(3)
         output_values(2)
         second_layer(3)

@@ -24,13 +24,13 @@ GROUPS = K1 // K_PASS
 SPANS = GROUPS // SPAN_PASSES
 UNIT_K = SPAN_PASSES * K_PASS
 WIDE_SPANS = 2
-LAST_SPANS = 2
+LAST_SPANS = 0
 RUN_UNITS = 2
 X_BUFS = 7
 VECTORS_BEHIND = 5
 SPREAD_RUN = 8
 WARM_BETWEEN = 3
-WARM_FIRST, WARM_LATER, WARM_LAST = 8, 4, 14
+WARM_FIRST, WARM_LATER, WARM_LAST = 6, 4, 16
 QUADRANTS = 4
 SLOPE = 0.01
 EPS = 1e-5
@@ -123,7 +123,7 @@ def tile_attention_prop_pa_k_kernel(
         ]
 
         x_runs, sorted_tiles, grouped_tiles, code_tiles = {}, {}, {}, {}
-        h1_tiles, biased_tiles = {}, {}
+        h1_tiles, biased_sums, biased_tiles = {}, {}, {}
 
         def load_scale_rows(plane, rows_per_quadrant, scale_rows):
             for quadrant in range(QUADRANTS):
@@ -150,7 +150,7 @@ def tile_attention_prop_pa_k_kernel(
             one, other = [order[n] for n in runs[r]]
             same_rows = one[0][0] == other[-1][0]
             same_groups = one[0][1] == other[0][1]
-            if r > 0 and (same_rows or same_groups):
+            if r > 1 and (same_rows or same_groups):
                 load_x(x_runs[r][:], runs[r])
             else:
                 for i, n in enumerate(runs[r]):
@@ -263,12 +263,14 @@ def tile_attention_prop_pa_k_kernel(
                     out=acc[a][:], lhsT=zeros[:, 0:P], rhs=zeros[:], start=True, stop=True
                 )
 
+        def hidden_sums(a):
+            biased_sums[a] = tail.tile([P, FEATS], F32, name="biased")
+            nc.vector.tensor_tensor(out=biased_sums[a][:], in0=acc[a][:], in1=b1_all[:], op=ALU.add)
+
         def hidden_values(a):
-            biased = tail.tile([P, FEATS], F32, name="biased")
-            nc.vector.tensor_tensor(out=biased[:], in0=acc[a][:], in1=b1_all[:], op=ALU.add)
             h1_tiles[a] = last.tile([P, FEATS], BF16, name="h1_rows")
             nc.vector.scalar_tensor_tensor(
-                out=h1_tiles[a][:], in0=biased[:], scalar=SLOPE, in1=biased[:],
+                out=h1_tiles[a][:], in0=biased_sums[a][:], scalar=SLOPE, in1=biased_sums[a][:],
                 op0=ALU.mult, op1=ALU.max,
             )
 
@@ -291,7 +293,7 @@ def tile_attention_prop_pa_k_kernel(
         def second_layer(a):
             rows = slice(a * P, (a + 1) * P)
             bank = banks.tile([P, FEAT_TILES, P], F32, name="h2_bank", tag="bank")
-            biased_tiles[a] = tail.tile([P, FEAT_TILES, P], F32, name="h2_biased")
+            biased_tiles[a] = last.tile([P, FEAT_TILES, P], F32, name="h2_biased")
             for j in range(FEAT_TILES):
                 nc.tensor.matmul_mx(
                     out=bank[:, j, :],
@@ -337,49 +339,54 @@ def tile_attention_prop_pa_k_kernel(
         for r in range(-2, len(runs)):
             for n in units_of(r + 2):
                 sort_words(n)
-            for a in closed_in(r - 2):
-                transpose_hidden(a)
             for n in units_of(r + 1):
                 transpose_x(n)
             if r == -1:
                 keep_busy(ROW_TILES - 1, WARM_LATER)
+            late = units_of(r + 1)[1:] if closed_in(r) else []
             for n in units_of(r + 1):
-                quantise_x(n)
-            for a in closed_in(r - 2):
-                quantise_hidden(a)
-            for a in closed_in(r - 3):
-                second_layer(a)
-                output_values(a)
-                row_tile_stats(a)
+                if n not in late:
+                    quantise_x(n)
             for n in units_of(r):
                 first_layer_passes(n)
-                if n == len(order) - RUN_UNITS:
-                    second_layer(1)
+                for a, g in order[n]:
+                    if g == GROUPS - 1:
+                        hidden_sums(a)
+                for m in late:
+                    quantise_x(m)
+                late = []
+            for a in closed_in(r) if r < len(runs) - 1 else []:
+                hidden_values(a)
             if r == SPREAD_RUN:
                 spread_b1()
             if r == SPREAD_RUN + 1:
                 spread_columns()
-            for a in closed_in(r):
-                hidden_values(a)
 
+        transpose_hidden(0)
+        transpose_hidden(1)
+        keep_busy(0, 2)
+        hidden_values(2)
+        quantise_hidden(0)
+        quantise_hidden(1)
+        hidden_values(3)
+        second_layer(0)
         transpose_hidden(2)
-        keep_busy(0, WARM_BETWEEN)
-        quantise_hidden(2)
-        output_values(1)
-        row_tile_stats(1)
         transpose_hidden(3)
-        second_layer(2)
-        keep_busy(0, WARM_BETWEEN)
+        second_layer(1)
+        output_values(0)
+        quantise_hidden(2)
         quantise_hidden(3)
-        output_values(2)
+        row_tile_stats(0)
+        keep_busy(0, 2)
+        second_layer(2)
         second_layer(3)
+        output_values(1)
+        output_values(2)
+        row_tile_stats(1)
+        output_values(3)
         row_tile_stats(2)
         keep_busy(0, WARM_LAST)
-        for j in range(FEAT_TILES + 1):
-            if j < FEAT_TILES:
-                output_values(3, slice(j, j + 1))
-            if j > 0:
-                row_tile_stats(3, [j - 1])
+        row_tile_stats(3)
 
         for j in range(FEAT_TILES):
             nc.vector.bn_aggr(

from contextlib import ExitStack

import concourse.mybir as mybir
from concourse.masks import make_identity

BF16 = mybir.dt.bfloat16
F32 = mybir.dt.float32
I32 = mybir.dt.int32
U32 = mybir.dt.uint32
U8 = mybir.dt.uint8
FP8X4 = mybir.dt.float8_e4m3fn_x4
ALU = mybir.AluOpType
ACT = mybir.ActivationFunctionType

P = 128
PACK = 4
K_PASS = P * PACK
ROWS, K1, FEATS = 512, 16384, 512
ROW_TILES = ROWS // P
FEAT_TILES = FEATS // P
HALF_FEATS = FEATS // 2
SPAN_PASSES = 4
GROUPS = K1 // K_PASS
SPANS = GROUPS // SPAN_PASSES
UNIT_K = SPAN_PASSES * K_PASS
WIDE_SPANS = 2
LAST_SPANS = 0
RUN_UNITS = 2
X_BUFS = 7
VECTORS_BEHIND = 5
SPREAD_RUN = 8
WARM_BETWEEN = 3
WARM_FIRST, WARM_LATER, WARM_LAST = 6, 4, 16
QUADRANTS = 4
SLOPE = 0.01
EPS = 1e-5
BN_STATS = 6

FLOPS = 2 * ROWS * K1 * FEATS + 2 * ROWS * FEATS * FEATS


def tile_attention_prop_pa_k_kernel(
    tc, x, w1_words, w1_scales, b1, w2_words, w2_scales, b2, gamma, beta, out
):
    nc = tc.nc

    def of_span(a, s):
        return [(a, s * SPAN_PASSES + i) for i in range(SPAN_PASSES)]

    order = [
        [(a + i, g + j) for i in range(2) for j in range(2)]
        for g in range(0, WIDE_SPANS * SPAN_PASSES, 2)
        for a in range(0, ROW_TILES, 2)
    ]
    order += [of_span(a, s) for s in range(WIDE_SPANS, SPANS - LAST_SPANS) for a in range(ROW_TILES)]
    order += [of_span(a, s) for a in range(ROW_TILES) for s in range(SPANS - LAST_SPANS, SPANS)]
    runs = [list(range(n, n + RUN_UNITS)) for n in range(0, len(order), RUN_UNITS)]

    weight_loads = [range(g, g + 2) for g in range(0, WIDE_SPANS * SPAN_PASSES, 2)]
    weight_loads += [
        range(s * SPAN_PASSES, (s + 1) * SPAN_PASSES) for s in range(WIDE_SPANS, SPANS)
    ]
    weights_behind = {}
    for groups in weight_loads:
        needed = min(n for n, unit in enumerate(order) if (unit[0][0], groups[0]) in unit)
        run = needed // RUN_UNITS + 1
        weights_behind[run] = weights_behind.get(run, []) + [groups]

    def units_of(r):
        return runs[r] if 0 <= r < len(runs) else []

    def closed_in(r):
        return [a for n in units_of(r) for a, g in order[n] if g == GROUPS - 1]

    with ExitStack() as ctx:
        const = ctx.enter_context(tc.tile_pool(name="const", bufs=1))
        x_pool = ctx.enter_context(tc.tile_pool(name="x", bufs=X_BUFS))
        sorted_pool = ctx.enter_context(tc.tile_pool(name="sorted", bufs=2 * RUN_UNITS))
        grouped_pool = ctx.enter_context(tc.tile_pool(name="grouped", bufs=2 * RUN_UNITS))
        codes_pool = ctx.enter_context(tc.tile_pool(name="codes", bufs=3 * RUN_UNITS))
        tail = ctx.enter_context(tc.tile_pool(name="tail", bufs=2))
        last = ctx.enter_context(tc.tile_pool(name="last", bufs=FEAT_TILES))
        sums = ctx.enter_context(tc.psum_pool(name="sums", bufs=1))
        banks = ctx.enter_context(tc.psum_pool(name="banks", bufs=4))
        ctx.enter_context(tc.manual_schedule())

        w1_tiles = [
            const.tile([P, SPAN_PASSES, PACK * FEATS], U8, name="w1_span%d" % s, align_bytes=256)
            for s in range(SPANS)
        ]
        w1_planes = [
            const.tile([P, FEATS], U8, name="w1_planes%d" % s, align_bytes=256)
            for s in range(SPANS)
        ]
        w2_tile = const.tile([P, PACK * FEATS], U8, name="w2_tile", align_bytes=256)
        w2_plane = const.tile([P, FEATS], U8, name="w2_plane", align_bytes=256)
        ident_f32 = const.tile([P, P], F32, name="ident_f32", align_bytes=256)
        ident_bf16 = const.tile([P, P], BF16, name="ident_bf16")
        zeros = const.tile([P, FEATS], BF16, name="zeros")
        ones = const.tile([P, P], BF16, name="ones")
        b1_row = const.tile([P, FEATS], BF16, name="b1_row")
        b1_all = const.tile([P, FEATS], F32, name="b1_all")
        vec_rows = const.tile([P, P], BF16, name="vec_rows")
        vec_cols = const.tile([P, 3 * FEAT_TILES], F32, name="vec_cols")
        b2_cols = vec_cols[:, 0:FEAT_TILES]
        gamma_cols = vec_cols[:, FEAT_TILES : 2 * FEAT_TILES]
        beta_cols = vec_cols[:, 2 * FEAT_TILES : 3 * FEAT_TILES]
        one_col = const.tile([P, 1], F32, name="one_col")
        root_col = const.tile([P, 1], F32, name="root_col")
        h1_grouped = const.tile([P, ROW_TILES, P, PACK], BF16, name="h1_grouped", align_bytes=256)
        h1_codes = const.tile([P, ROWS], U32, name="h1_codes", align_bytes=256)
        h1_scales = const.tile([P, ROWS], U8, name="h1_scales", align_bytes=256)
        h2 = const.tile([P, FEAT_TILES, ROWS], F32, name="h2")
        stats = const.tile([P, FEAT_TILES, ROW_TILES, BN_STATS], F32, name="stats")
        mean_var = const.tile([P, FEAT_TILES, 2], F32, name="mean_var")
        mean_gamma = const.tile([P, FEAT_TILES], F32, name="mean_gamma")
        rstd = const.tile([P, FEAT_TILES], F32, name="rstd")
        gain = const.tile([P, FEAT_TILES], F32, name="gain")
        mean_gain = const.tile([P, FEAT_TILES], F32, name="mean_gain")
        shift = const.tile([P, FEAT_TILES], F32, name="shift")
        acc = [
            sums.tile([P, FEATS], F32, name="acc%d" % a, tag="sum%d" % a) for a in range(ROW_TILES)
        ]

        x_runs, sorted_tiles, grouped_tiles, code_tiles = {}, {}, {}, {}
        h1_tiles, biased_sums, biased_tiles = {}, {}, {}

        def load_scale_rows(plane, rows_per_quadrant, scale_rows):
            for quadrant in range(QUADRANTS):
                first = 32 * quadrant
                nc.sync.dma_start(
                    out=plane[first : first + rows_per_quadrant, :].bitcast(I32),
                    in_=scale_rows(quadrant).bitcast(I32),
                )

        def load_x(tile, units):
            pairs = [pair for n in units for pair in order[n]]
            first, last_row = pairs[0][0], pairs[-1][0]
            k = slice(pairs[0][1] * K_PASS, (pairs[-1][1] + 1) * K_PASS)
            if first == last_row:
                nc.sync.dma_start(out=tile, in_=x[first * P : (first + 1) * P, k])
            else:
                nc.sync.dma_start(
                    out=tile.rearrange("p (a k) -> p a k", a=last_row - first + 1),
                    in_=x[first * P : (last_row + 1) * P, k].rearrange("(a m) k -> m a k", m=P),
                )

        def load_run(r):
            x_runs[r] = x_pool.tile([P, RUN_UNITS * UNIT_K], BF16, name="x_run")
            one, other = [order[n] for n in runs[r]]
            same_rows = one[0][0] == other[-1][0]
            same_groups = one[0][1] == other[0][1]
            if r > 1 and (same_rows or same_groups):
                load_x(x_runs[r][:], runs[r])
            else:
                for i, n in enumerate(runs[r]):
                    load_x(x_runs[r][:, i * UNIT_K : (i + 1) * UNIT_K], [n])
            for groups in weights_behind.get(r, []):
                load_weights(groups)
            if r == VECTORS_BEHIND:
                load_vectors()
            if r == len(runs) - 1:
                load_scale_rows(
                    w2_plane, 4, lambda quadrant: w2_scales[0, 4 * quadrant : 4 * quadrant + 4, :]
                )
                nc.sync.dma_start(
                    out=w2_tile[:].bitcast(I32),
                    in_=w2_words[0].rearrange("p n t -> p (n t)").bitcast(I32),
                )

        def load_vectors():
            nc.sync.dma_start(out=b1_row[0:1, :], in_=b1.rearrange("(o f) -> o f", o=1))
            for i, vector in enumerate((b2, gamma, beta)):
                nc.sync.dma_start(
                    out=vec_rows[i * FEAT_TILES : (i + 1) * FEAT_TILES, :],
                    in_=vector.rearrange("(j p) -> j p", p=P),
                )

        def load_weights(groups):
            s, first = divmod(groups[0], SPAN_PASSES)
            if first == 0:
                span = slice(s * SPAN_PASSES, (s + 1) * SPAN_PASSES)
                load_scale_rows(
                    w1_planes[s],
                    4 * SPAN_PASSES,
                    lambda quadrant: w1_scales[span, 4 * quadrant : 4 * quadrant + 4, :],
                )
            nc.sync.dma_start(
                out=w1_tiles[s][:, first : first + len(groups), :].bitcast(I32),
                in_=w1_words[groups[0] : groups[-1] + 1]
                .rearrange("g p n t -> p g (n t)")
                .bitcast(I32),
            )

        def sort_words(n):
            sorted_tiles[n] = sorted_pool.tile(
                [P, SPAN_PASSES, 2, P], F32, name="sorted_words", align_bytes=256
            )
            nc.vector.tensor_copy(
                out=sorted_tiles[n][:],
                in_=x_runs[n // RUN_UNITS][:, (n % RUN_UNITS) * UNIT_K : (n % RUN_UNITS + 1) * UNIT_K]
                .bitcast(F32)
                .rearrange("p (j w u) -> p j u w", j=SPAN_PASSES, u=2),
            )
            r = n // RUN_UNITS + X_BUFS
            if n % RUN_UNITS == RUN_UNITS - 1 and r < len(runs):
                load_run(r)

        def transpose_x(n):
            grouped_tiles[n] = grouped_pool.tile([P, UNIT_K], BF16, name="grouped", align_bytes=256)
            words = grouped_tiles[n][:].bitcast(F32).rearrange(
                "p (j m u) -> p j m u", j=SPAN_PASSES, u=2
            )
            for half in range(SPAN_PASSES // 2):
                bank = banks.tile([P, 2, 2, P], F32, name="x_bank", tag="bank")
                for jj in range(2):
                    for u in range(2):
                        nc.tensor.transpose(
                            out=bank[:, jj, u, :],
                            in_=sorted_tiles[n][:, 2 * half + jj, u, :],
                            identity=ident_f32[:],
                        )
                nc.scalar.copy(
                    out=words[:, 2 * half : 2 * half + 2],
                    in_=bank[:].rearrange("p j u m -> p j m u"),
                )

        def quantise_x(n):
            codes = codes_pool.tile([P, SPAN_PASSES * P], U32, name="x_codes", align_bytes=256)
            scales = codes_pool.tile([P, SPAN_PASSES * P], U8, name="x_scales", align_bytes=256)
            nc.vector.quantize_mx(
                out=codes[:].bitcast(FP8X4), scales=scales[:], in_=grouped_tiles[n][:]
            )
            code_tiles[n] = (codes, scales)

        def first_layer_passes(n):
            codes, scales = code_tiles[n]
            for i, (a, g) in enumerate(order[n]):
                rows = slice(i * P, (i + 1) * P)
                s, j = divmod(g, SPAN_PASSES)
                nc.tensor.matmul_mx(
                    out=acc[a][:],
                    lhsT=codes[:, rows].bitcast(FP8X4),
                    lhsT_scale=scales[:, rows],
                    rhs=w1_tiles[s][:, j, :].bitcast(FP8X4),
                    rhs_scale=w1_planes[s][4 * j : P, :],
                    start=(g == 0),
                    stop=(g == GROUPS - 1),
                )

        def spread_b1():
            b1_bank = banks.tile([P, FEATS], F32, name="b1_bank", tag="bank")
            nc.tensor.matmul(out=b1_bank[:], lhsT=ones[:], rhs=b1_row[:], start=True, stop=True)
            nc.scalar.copy(out=b1_all[:], in_=b1_bank[:])
        def spread_columns():
            vec_bank = banks.tile([P, P], BF16, name="vec_bank", tag="bank")
            nc.tensor.transpose(out=vec_bank[:], in_=vec_rows[:], identity=ident_bf16[:])
            nc.vector.tensor_copy(out=vec_cols[:], in_=vec_bank[:, 0 : 3 * FEAT_TILES])

        def keep_busy(a, count):
            for i in range(count):
                nc.tensor.matmul(
                    out=acc[a][:], lhsT=zeros[:, 0:P], rhs=zeros[:], start=True, stop=True
                )

        def hidden_sums(a):
            biased_sums[a] = tail.tile([P, FEATS], F32, name="biased")
            nc.vector.tensor_tensor(out=biased_sums[a][:], in0=acc[a][:], in1=b1_all[:], op=ALU.add)

        def hidden_values(a):
            h1_tiles[a] = last.tile([P, FEATS], BF16, name="h1_rows")
            nc.vector.scalar_tensor_tensor(
                out=h1_tiles[a][:], in0=biased_sums[a][:], scalar=SLOPE, in1=biased_sums[a][:],
                op0=ALU.mult, op1=ALU.max,
            )

        def transpose_hidden(a):
            bank = banks.tile([P, PACK, P], BF16, name="h1_bank", tag="bank")
            for t in range(PACK):
                nc.tensor.transpose(
                    out=bank[:, t, :], in_=h1_tiles[a][:, t:FEATS:PACK], identity=ident_bf16[:]
                )
            nc.scalar.copy(out=h1_grouped[:, a], in_=bank[:].rearrange("p t m -> p m t"))

        def quantise_hidden(a):
            rows = slice(a * P, (a + 1) * P)
            nc.vector.quantize_mx(
                out=h1_codes[:, rows].bitcast(FP8X4),
                scales=h1_scales[:, rows],
                in_=h1_grouped[:, a].rearrange("p m t -> p (m t)"),
            )

        def second_layer(a):
            rows = slice(a * P, (a + 1) * P)
            bank = banks.tile([P, FEAT_TILES, P], F32, name="h2_bank", tag="bank")
            biased_tiles[a] = last.tile([P, FEAT_TILES, P], F32, name="h2_biased")
            for j in range(FEAT_TILES):
                nc.tensor.matmul_mx(
                    out=bank[:, j, :],
                    lhsT=w2_tile[:, j * PACK * P : (j + 1) * PACK * P].bitcast(FP8X4),
                    lhsT_scale=w2_plane[:, j * P : (j + 1) * P],
                    rhs=h1_codes[:, rows].bitcast(FP8X4),
                    rhs_scale=h1_scales[:, rows],
                    start=True,
                    stop=True,
                )
            for j in range(FEAT_TILES):
                nc.scalar.activation(
                    out=biased_tiles[a][:, j, :], in_=bank[:, j, :], func=ACT.Identity,
                    bias=b2_cols[:, j : j + 1], scale=1.0,
                )

        def output_values(a, tiles=slice(0, FEAT_TILES)):
            biased = biased_tiles[a][:, tiles, :]
            nc.vector.scalar_tensor_tensor(
                out=h2[:, tiles, a * P : (a + 1) * P], in0=biased, scalar=SLOPE, in1=biased,
                op0=ALU.mult, op1=ALU.max,
            )

        def row_tile_stats(a, tiles=range(FEAT_TILES)):
            for j in tiles:
                nc.vector.bn_stats(out=stats[:, j, a, :], in_=h2[:, j, a * P : (a + 1) * P])

        nc.vector.memset(zeros[:], 0.0)
        for plane in w1_planes + [w2_plane]:
            nc.vector.memset(plane[:].bitcast(I32), 0)
        nc.vector.memset(b1_row[:], 0.0)
        nc.vector.memset(vec_rows[:], 0.0)
        nc.vector.memset(ones[:], 1.0)
        nc.vector.memset(one_col[:], 1.0)
        make_identity(nc, ident_f32[:])
        make_identity(nc, ident_bf16[:])

        for r in range(X_BUFS):
            load_run(r)
        keep_busy(ROW_TILES - 1, WARM_FIRST)
        nc.scalar.activation(out=root_col[:], in_=one_col[:], func=ACT.Abs_reciprocal_sqrt)

        for r in range(-2, len(runs)):
            for n in units_of(r + 2):
                sort_words(n)
            for n in units_of(r + 1):
                transpose_x(n)
            if r == -1:
                keep_busy(ROW_TILES - 1, WARM_LATER)
            late = units_of(r + 1)[1:] if closed_in(r) else []
            for n in units_of(r + 1):
                if n not in late:
                    quantise_x(n)
            for n in units_of(r):
                first_layer_passes(n)
                for a, g in order[n]:
                    if g == GROUPS - 1:
                        hidden_sums(a)
                for m in late:
                    quantise_x(m)
                late = []
            for a in closed_in(r) if r < len(runs) - 1 else []:
                hidden_values(a)
            if r == SPREAD_RUN:
                spread_b1()
            if r == SPREAD_RUN + 1:
                spread_columns()

        transpose_hidden(0)
        transpose_hidden(1)
        keep_busy(0, 2)
        hidden_values(2)
        quantise_hidden(0)
        quantise_hidden(1)
        hidden_values(3)
        second_layer(0)
        transpose_hidden(2)
        transpose_hidden(3)
        second_layer(1)
        output_values(0)
        quantise_hidden(2)
        quantise_hidden(3)
        row_tile_stats(0)
        keep_busy(0, 2)
        second_layer(2)
        second_layer(3)
        output_values(1)
        output_values(2)
        row_tile_stats(1)
        output_values(3)
        row_tile_stats(2)
        keep_busy(0, WARM_LAST)
        row_tile_stats(3)

        for j in range(FEAT_TILES):
            nc.vector.bn_aggr(
                out=mean_var[:, j, :], in_=stats[:, j].rearrange("p h c -> p (h c)")
            )
        nc.scalar.activation(
            out=rstd[:], in_=mean_var[:, :, 1], func=ACT.Abs_reciprocal_sqrt, bias=EPS, scale=1.0
        )
        nc.vector.tensor_tensor(out=mean_gamma[:], in0=mean_var[:, :, 0], in1=gamma_cols, op=ALU.mult)
        nc.vector.tensor_tensor(out=mean_gain[:], in0=mean_gamma[:], in1=rstd[:], op=ALU.mult)
        nc.vector.tensor_tensor(out=gain[:], in0=gamma_cols, in1=rstd[:], op=ALU.mult)
        nc.vector.tensor_tensor(out=shift[:], in0=beta_cols, in1=mean_gain[:], op=ALU.subtract)

        normed = const.tile([P, FEAT_TILES, ROWS], F32, name="normed")
        for a in range(ROW_TILES):
            rows = slice(a * P, (a + 1) * P)
            for j in range(FEAT_TILES):
                if j == FEAT_TILES - 1:
                    nc.scalar.activation(
                        out=normed[:, j, rows], in_=h2[:, j, rows], func=ACT.Identity,
                        scale=gain[:, j : j + 1], bias=shift[:, j : j + 1],
                    )
                else:
                    nc.vector.tensor_scalar(
                        out=normed[:, j, rows], in0=h2[:, j, rows],
                        scalar1=gain[:, j : j + 1], scalar2=shift[:, j : j + 1],
                        op0=ALU.mult, op1=ALU.add,
                    )
        for a in range(ROW_TILES):
            out_rows = last.tile([P, 2, HALF_FEATS], F32, name="out_rows")
            for half in range(2):
                if half:
                    out_bank = banks.tile([P, FEAT_TILES // 2, P], F32, name="out_bank_b", tag="bank")
                else:
                    out_bank = sums.tile([P, FEAT_TILES // 2, P], F32, name="out_bank_a", tag="sum%d" % a)
                for i in range(FEAT_TILES // 2):
                    nc.tensor.transpose(
                        out=out_bank[:, i, :],
                        in_=normed[:, half * FEAT_TILES // 2 + i, a * P : (a + 1) * P],
                        identity=ident_f32[:],
                    )
                copy = nc.vector.tensor_copy if half else nc.scalar.copy
                copy(out=out_rows[:, half, :], in_=out_bank[:].rearrange("p j f -> p (j f)"))
            nc.sync.dma_start(
                out=out[a * P : (a + 1) * P, :], in_=out_rows[:].rearrange("p h f -> p (h f)")
            )
